import numpy as np
import ml_dtypes

BF16 = ml_dtypes.bfloat16


def bf(x):
    return np.asarray(x, np.float32).astype(BF16)


def f32(x):
    return np.asarray(x, np.float32)


def f64(x):
    return np.asarray(x).astype(np.float64)


def striped(idx):
    return np.tile(idx.reshape(-1, 16).T, (8, 1))


K, SH, D, S, N = 128, 4, 128, 4096, 2048
ALPHA = 100.0
SHARP = 5.0


def setup_inputs():
    x = bf(np.random.standard_normal((D, N)))
    centre = np.random.standard_normal((K, 1, D))
    shadow = np.random.standard_normal((K, SH, D))
    spread = 0.5 + np.random.random_sample((K, SH, 1))
    centroids = bf(SHARP / (2.0 * ALPHA * np.sqrt(2.0 * D)) * spread * (centre + shadow))
    base = f32(1.0 + 0.5 * np.random.random_sample((K, S)))
    return {"x": x, "centroids": centroids, "base": base, "offs": striped(np.random.permutation(S)[:N])}


def reference(x, centroids, base, offs):
    idx = offs[:16].T.reshape(-1)
    c = f64(centroids).reshape(K * SH, D)
    z = 2.0 * ALPHA * (c @ f64(x)) - ALPHA * np.sqrt(np.sum(c * c, axis=1, keepdims=True))
    e = np.exp(z)
    over_clusters = (np.ones((K, K)) @ e.reshape(K, SH * N)).reshape(K, SH, N)
    e = e.reshape(K, SH, N)
    over_shadows = np.sum(e, axis=1, keepdims=True)
    f = 1.0 + (e / over_clusters) * (e / over_shadows)
    half = SH // 2
    a = np.prod(f[:, :half], axis=1)
    b = np.prod(f[:, half:], axis=1)
    out = f64(base).copy()
    out[:, idx] = a * b
    return out

@@ -1,0 +1,169 @@
+import concourse.mybir as mybir
+from concourse.masks import make_identity
+
+F32 = mybir.dt.float32
+BF16 = mybir.dt.bfloat16
+U16 = mybir.dt.uint16
+ALU = mybir.AluOpType
+ACT = mybir.ActivationFunctionType
+FREE_AXIS = mybir.AxisListType.X
+
+K, SH, D, S, N = 128, 4, 128, 4096, 2048
+ALPHA = 100.0
+P = 128
+GB = 4
+GROUPS = N // (GB * P)
+PIECE = 1024
+GROUPS_IN_PIECE = PIECE // (GB * P)
+LIFT = 2.0**32
+
+FLOPS = 2 * K * SH * D * N
+
+
+def tile_sralnet_kernel(tc, x, centroids, base, offs, out):
+    nc = tc.nc
+    with (
+        tc.tile_pool(name="held", bufs=1) as held,
+        tc.tile_pool(name="work", bufs=2) as work,
+        tc.tile_pool(name="stats", bufs=2) as stats,
+        tc.psum_pool(name="setup_psum", bufs=1) as setup_psum,
+        tc.psum_pool(name="z_psum", bufs=3) as z_psum,
+        tc.psum_pool(name="turned_psum", bufs=2) as turned_psum,
+    ):
+        offsets = held.tile([P, N // 16], U16, name="offsets")
+        nc.sync.dma_start(offsets[:], offs)
+        cents = held.tile([K, SH, D], BF16, name="cents")
+        nc.sync.dma_start(cents[:], centroids)
+        pixels = held.tile([D, N], BF16, name="pixels")
+        for g in range(GROUPS):
+            cols = slice(g * GB * P, (g + 1) * GB * P)
+            nc.sync.dma_start(pixels[:, cols], x[:, cols])
+        window = held.tile([K, S], F32, name="window")
+        nc.sync.dma_start(window[:], base)
+
+        ident_f = held.tile([P, P], F32, name="ident_f")
+        make_identity(nc, ident_f[:])
+        ident_b = held.tile([P, P], BF16, name="ident_b")
+        nc.vector.tensor_copy(ident_b[:], ident_f[:])
+        ones_b = held.tile([P, P], BF16, name="ones_b")
+        nc.vector.memset(ones_b[:], 1.0)
+        half = held.tile([K, SH], F32, name="half")
+        nc.vector.memset(half[:], 0.5)
+
+        cents_t_ps = setup_psum.tile([D, SH * K], BF16, name="cents_t_ps", tag="setup")
+        for i in range(SH):
+            nc.tensor.transpose(cents_t_ps[:, i * K : (i + 1) * K], cents[:, i, :], ident_b[:])
+        cents_t = held.tile([D, SH * K], BF16, name="cents_t")
+        nc.vector.tensor_copy(cents_t[:], cents_t_ps[:])
+
+        squares = held.tile([K, SH, D], F32, name="squares")
+        nc.vector.tensor_tensor(squares[:], cents[:], cents[:], ALU.mult)
+        sumsq = held.tile([K, SH], F32, name="sumsq")
+        nc.vector.tensor_reduce(sumsq[:], squares[:], FREE_AXIS, ALU.add)
+        norm = held.tile([K, SH], F32, name="norm")
+        nc.gpsimd.tensor_tensor(norm[:], sumsq[:], half[:], ALU.pow)
+        shift = held.tile([K, SH], F32, name="shift")
+        nc.vector.tensor_scalar_mul(shift[:], norm[:], -0.5)
+
+        pieces = held.tile([K, SH, P], BF16, name="pieces")
+        nc.vector.memset(pieces[:], 0.0)
+        rest = held.tile([K, SH], F32, name="rest")
+        nc.vector.tensor_copy(pieces[:, :, 0], shift[:])
+        nc.vector.tensor_tensor(rest[:], shift[:], pieces[:, :, 0], ALU.subtract)
+        nc.vector.tensor_copy(pieces[:, :, 1], rest[:])
+        nc.vector.tensor_tensor(pieces[:, :, 2], rest[:], pieces[:, :, 1], ALU.subtract)
+        rows_ps = setup_psum.tile([P, SH * K], BF16, name="rows_ps", tag="setup")
+        for i in range(SH):
+            nc.tensor.transpose(rows_ps[:, i * K : (i + 1) * K], pieces[:, i, :], ident_b[:])
+        rows = held.tile([P, SH * K], BF16, name="rows")
+        nc.vector.tensor_copy(rows[:], rows_ps[:])
+
+        factors = [
+            [held.tile([K, PIECE], F32, name=f"factor{piece}{h}") for h in range(2)]
+            for piece in range(N // PIECE)
+        ]
+
+        for g in range(GROUPS):
+            e = work.tile([P, GB, SH, K], F32, name="e")
+            sum_q = stats.tile([P, GB * SH], F32, name="sum_q")
+            for b in range(GB):
+                first = (g * GB + b) * P
+                z = z_psum.tile([P, SH * K], F32, name="z")
+                nc.tensor.matmul(z[:], pixels[:, first : first + P], cents_t[:], start=True, stop=False)
+                nc.tensor.matmul(z[:], ones_b[:], rows[:], start=False, stop=True)
+                for i in range(SH):
+                    nc.scalar.activation(
+                        e[:, b, i, :],
+                        z[:, i * K : (i + 1) * K],
+                        ACT.Exp,
+                        scale=2.0 * ALPHA,
+                        accum_out=sum_q[:, b * SH + i : b * SH + i + 1],
+                    )
+
+            pair01 = work.tile([P, GB, K], F32, name="pair01")
+            nc.gpsimd.tensor_tensor(pair01[:], e[:, :, 0, :], e[:, :, 1, :], ALU.add)
+            pair23 = work.tile([P, GB, K], F32, name="pair23")
+            nc.gpsimd.tensor_tensor(pair23[:], e[:, :, 2, :], e[:, :, 3, :], ALU.add)
+            sum_r = work.tile([P, GB, K], F32, name="sum_r")
+            nc.gpsimd.tensor_tensor(sum_r[:], pair01[:], pair23[:], ALU.add)
+
+            recip_q = stats.tile([P, GB * SH], F32, name="recip_q")
+            nc.vector.reciprocal(recip_q[:], sum_q[:])
+
+            total = stats.tile([P, GB], F32, name="total")
+            nc.vector.tensor_reduce(
+                total[:], sum_q[:].rearrange("p (b i) -> p b i", i=SH), FREE_AXIS, ALU.add
+            )
+            lift = stats.tile([P, GB], F32, name="lift")
+            nc.vector.reciprocal(lift[:], total[:])
+            nc.vector.tensor_scalar_mul(lift[:], lift[:], LIFT)
+            log_r = work.tile([P, GB, K], F32, name="log_r")
+            for b in range(GB):
+                nc.scalar.activation(log_r[:, b, :], sum_r[:, b, :], ACT.Ln, scale=lift[:, b : b + 1])
+            recip_r = work.tile([P, GB, K], F32, name="recip_r")
+            nc.scalar.activation(recip_r[:], log_r[:], ACT.Exp, scale=-1.0)
+            for b in range(GB):
+                nc.vector.tensor_scalar_mul(recip_r[:, b, :], recip_r[:, b, :], lift[:, b : b + 1])
+
+            weighted = work.tile([P, GB, SH, K], F32, name="weighted")
+            for b in range(GB):
+                for i in range(SH):
+                    nc.vector.scalar_tensor_tensor(
+                        weighted[:, b, i, :],
+                        e[:, b, i, :],
+                        recip_q[:, b * SH + i : b * SH + i + 1],
+                        e[:, b, i, :],
+                        ALU.mult,
+                        ALU.mult,
+                    )
+            sa = work.tile([P, GB, SH, K], F32, name="sa")
+            nc.gpsimd.tensor_tensor(
+                sa[:], weighted[:], recip_r[:].unsqueeze(2).to_broadcast([P, GB, SH, K]), ALU.mult
+            )
+
+            sa_pairs = sa[:].rearrange("p b (h t) k -> p b h t k", t=2)
+            odd = work.tile([P, GB, 2, K], F32, name="odd")
+            nc.gpsimd.tensor_scalar_add(odd[:], sa_pairs[:, :, :, 1, :], 1.0)
+            halves = work.tile([P, GB, 2, K], F32, name="halves")
+            nc.vector.scalar_tensor_tensor(
+                halves[:], sa_pairs[:, :, :, 0, :], 1.0, odd[:], ALU.add, ALU.mult
+            )
+
+            piece = g // GROUPS_IN_PIECE
+            at = (g % GROUPS_IN_PIECE) * GB * P
+            for h in range(2):
+                turned = turned_psum.tile([K, GB * P], F32, name=f"turned{h}")
+                for b in range(GB):
+                    nc.tensor.transpose(turned[:, b * P : (b + 1) * P], halves[:, b, h, :], ident_f[:])
+                nc.scalar.copy(factors[piece][h][:, at : at + GB * P], turned[:])
+
+            if g % GROUPS_IN_PIECE == GROUPS_IN_PIECE - 1:
+                list_cols = slice(piece * PIECE // 16, (piece + 1) * PIECE // 16)
+                nc.vector.tensor_tensor(
+                    window[:].indirect(offsets[:, list_cols]),
+                    factors[piece][0][:],
+                    factors[piece][1][:],
+                    ALU.mult,
+                )
+
+        nc.sync.dma_start(out, window[:])

@@ -24,8 +24,8 @@ def tile_sralnet_kernel(tc, x, centroids, base, offs, out):
     nc = tc.nc
     with (
         tc.tile_pool(name="held", bufs=1) as held,
-        tc.tile_pool(name="work", bufs=2) as work,
-        tc.tile_pool(name="stats", bufs=2) as stats,
+        tc.tile_pool(name="work", bufs=3) as work,
+        tc.tile_pool(name="stats", bufs=3) as stats,
         tc.psum_pool(name="setup_psum", bufs=1) as setup_psum,
         tc.psum_pool(name="z_psum", bufs=3) as z_psum,
         tc.psum_pool(name="turned_psum", bufs=2) as turned_psum,
@@ -120,10 +120,8 @@ def tile_sralnet_kernel(tc, x, centroids, base, offs, out):
             log_r = work.tile([P, GB, K], F32, name="log_r")
             for b in range(GB):
                 nc.scalar.activation(log_r[:, b, :], sum_r[:, b, :], ACT.Ln, scale=lift[:, b : b + 1])
-            recip_r = work.tile([P, GB, K], F32, name="recip_r")
-            nc.scalar.activation(recip_r[:], log_r[:], ACT.Exp, scale=-1.0)
-            for b in range(GB):
-                nc.vector.tensor_scalar_mul(recip_r[:, b, :], recip_r[:, b, :], lift[:, b : b + 1])
+            recip_lifted = work.tile([P, GB, K], F32, name="recip_lifted")
+            nc.scalar.activation(recip_lifted[:], log_r[:], ACT.Exp, scale=-1.0)
 
             weighted = work.tile([P, GB, SH, K], F32, name="weighted")
             for b in range(GB):
@@ -137,13 +135,19 @@ def tile_sralnet_kernel(tc, x, centroids, base, offs, out):
                         ALU.mult,
                     )
             sa = work.tile([P, GB, SH, K], F32, name="sa")
-            nc.gpsimd.tensor_tensor(
-                sa[:], weighted[:], recip_r[:].unsqueeze(2).to_broadcast([P, GB, SH, K]), ALU.mult
-            )
+            for b in range(GB):
+                nc.vector.scalar_tensor_tensor(
+                    sa[:, b, :, :],
+                    weighted[:, b, :, :],
+                    lift[:, b : b + 1],
+                    recip_lifted[:, b, :].unsqueeze(1).to_broadcast([P, SH, K]),
+                    ALU.mult,
+                    ALU.mult,
+                )
 
             sa_pairs = sa[:].rearrange("p b (h t) k -> p b h t k", t=2)
             odd = work.tile([P, GB, 2, K], F32, name="odd")
-            nc.gpsimd.tensor_scalar_add(odd[:], sa_pairs[:, :, :, 1, :], 1.0)
+            nc.vector.tensor_scalar_add(odd[:], sa_pairs[:, :, :, 1, :], 1.0)
             halves = work.tile([P, GB, 2, K], F32, name="halves")
             nc.vector.scalar_tensor_tensor(
                 halves[:], sa_pairs[:, :, :, 0, :], 1.0, odd[:], ALU.add, ALU.mult

@@ -24,8 +24,8 @@ def tile_sralnet_kernel(tc, x, centroids, base, offs, out):
     nc = tc.nc
     with (
         tc.tile_pool(name="held", bufs=1) as held,
-        tc.tile_pool(name="work", bufs=3) as work,
-        tc.tile_pool(name="stats", bufs=3) as stats,
+        tc.tile_pool(name="work", bufs=4) as work,
+        tc.tile_pool(name="stats", bufs=4) as stats,
         tc.psum_pool(name="setup_psum", bufs=1) as setup_psum,
         tc.psum_pool(name="z_psum", bufs=3) as z_psum,
         tc.psum_pool(name="turned_psum", bufs=2) as turned_psum,
@@ -83,91 +83,100 @@ def tile_sralnet_kernel(tc, x, centroids, base, offs, out):
             for piece in range(N // PIECE)
         ]
 
-        for g in range(GROUPS):
-            e = work.tile([P, GB, SH, K], F32, name="e")
-            sum_q = stats.tile([P, GB * SH], F32, name="sum_q")
-            for b in range(GB):
-                first = (g * GB + b) * P
-                z = z_psum.tile([P, SH * K], F32, name="z")
-                nc.tensor.matmul(z[:], pixels[:, first : first + P], cents_t[:], start=True, stop=False)
-                nc.tensor.matmul(z[:], ones_b[:], rows[:], start=False, stop=True)
-                for i in range(SH):
-                    nc.scalar.activation(
-                        e[:, b, i, :],
-                        z[:, i * K : (i + 1) * K],
-                        ACT.Exp,
-                        scale=2.0 * ALPHA,
-                        accum_out=sum_q[:, b * SH + i : b * SH + i + 1],
-                    )
+        for piece in range(N // PIECE):
+            groups = range(piece * GROUPS_IN_PIECE, (piece + 1) * GROUPS_IN_PIECE)
+            e, sum_q, sum_r, recip_q, lift, log_r, recip_lifted, weighted = {}, {}, {}, {}, {}, {}, {}, {}
 
-            pair01 = work.tile([P, GB, K], F32, name="pair01")
-            nc.gpsimd.tensor_tensor(pair01[:], e[:, :, 0, :], e[:, :, 1, :], ALU.add)
-            pair23 = work.tile([P, GB, K], F32, name="pair23")
-            nc.gpsimd.tensor_tensor(pair23[:], e[:, :, 2, :], e[:, :, 3, :], ALU.add)
-            sum_r = work.tile([P, GB, K], F32, name="sum_r")
-            nc.gpsimd.tensor_tensor(sum_r[:], pair01[:], pair23[:], ALU.add)
-
-            recip_q = stats.tile([P, GB * SH], F32, name="recip_q")
-            nc.vector.reciprocal(recip_q[:], sum_q[:])
-
-            total = stats.tile([P, GB], F32, name="total")
-            nc.vector.tensor_reduce(
-                total[:], sum_q[:].rearrange("p (b i) -> p b i", i=SH), FREE_AXIS, ALU.add
-            )
-            lift = stats.tile([P, GB], F32, name="lift")
-            nc.vector.reciprocal(lift[:], total[:])
-            nc.vector.tensor_scalar_mul(lift[:], lift[:], LIFT)
-            log_r = work.tile([P, GB, K], F32, name="log_r")
-            for b in range(GB):
-                nc.scalar.activation(log_r[:, b, :], sum_r[:, b, :], ACT.Ln, scale=lift[:, b : b + 1])
-            recip_lifted = work.tile([P, GB, K], F32, name="recip_lifted")
-            nc.scalar.activation(recip_lifted[:], log_r[:], ACT.Exp, scale=-1.0)
-
-            weighted = work.tile([P, GB, SH, K], F32, name="weighted")
-            for b in range(GB):
-                for i in range(SH):
-                    nc.vector.scalar_tensor_tensor(
-                        weighted[:, b, i, :],
-                        e[:, b, i, :],
-                        recip_q[:, b * SH + i : b * SH + i + 1],
-                        e[:, b, i, :],
-                        ALU.mult,
-                        ALU.mult,
-                    )
-            sa = work.tile([P, GB, SH, K], F32, name="sa")
-            for b in range(GB):
-                nc.vector.scalar_tensor_tensor(
-                    sa[:, b, :, :],
-                    weighted[:, b, :, :],
-                    lift[:, b : b + 1],
-                    recip_lifted[:, b, :].unsqueeze(1).to_broadcast([P, SH, K]),
-                    ALU.mult,
-                    ALU.mult,
-                )
-
-            sa_pairs = sa[:].rearrange("p b (h t) k -> p b h t k", t=2)
-            odd = work.tile([P, GB, 2, K], F32, name="odd")
-            nc.vector.tensor_scalar_add(odd[:], sa_pairs[:, :, :, 1, :], 1.0)
-            halves = work.tile([P, GB, 2, K], F32, name="halves")
-            nc.vector.scalar_tensor_tensor(
-                halves[:], sa_pairs[:, :, :, 0, :], 1.0, odd[:], ALU.add, ALU.mult
-            )
-
-            piece = g // GROUPS_IN_PIECE
-            at = (g % GROUPS_IN_PIECE) * GB * P
-            for h in range(2):
-                turned = turned_psum.tile([K, GB * P], F32, name=f"turned{h}")
+            for g in groups:
+                e[g] = work.tile([P, GB, SH, K], F32, name="e")
+                sum_q[g] = stats.tile([P, GB * SH], F32, name="sum_q")
                 for b in range(GB):
-                    nc.tensor.transpose(turned[:, b * P : (b + 1) * P], halves[:, b, h, :], ident_f[:])
-                nc.scalar.copy(factors[piece][h][:, at : at + GB * P], turned[:])
+                    first = (g * GB + b) * P
+                    z = z_psum.tile([P, SH * K], F32, name="z")
+                    nc.tensor.matmul(z[:], pixels[:, first : first + P], cents_t[:], start=True, stop=False)
+                    nc.tensor.matmul(z[:], ones_b[:], rows[:], start=False, stop=True)
+                    for i in range(SH):
+                        nc.scalar.activation(
+                            e[g][:, b, i, :],
+                            z[:, i * K : (i + 1) * K],
+                            ACT.Exp,
+                            scale=2.0 * ALPHA,
+                            accum_out=sum_q[g][:, b * SH + i : b * SH + i + 1],
+                        )
 
-            if g % GROUPS_IN_PIECE == GROUPS_IN_PIECE - 1:
-                list_cols = slice(piece * PIECE // 16, (piece + 1) * PIECE // 16)
-                nc.vector.tensor_tensor(
-                    window[:].indirect(offsets[:, list_cols]),
-                    factors[piece][0][:],
-                    factors[piece][1][:],
-                    ALU.mult,
+            for g in groups:
+                pair01 = work.tile([P, GB, K], F32, name="pair01")
+                nc.gpsimd.tensor_tensor(pair01[:], e[g][:, :, 0, :], e[g][:, :, 1, :], ALU.add)
+                pair23 = work.tile([P, GB, K], F32, name="pair23")
+                nc.gpsimd.tensor_tensor(pair23[:], e[g][:, :, 2, :], e[g][:, :, 3, :], ALU.add)
+                sum_r[g] = work.tile([P, GB, K], F32, name="sum_r")
+                nc.gpsimd.tensor_tensor(sum_r[g][:], pair01[:], pair23[:], ALU.add)
+
+                recip_q[g] = stats.tile([P, GB * SH], F32, name="recip_q")
+                nc.vector.reciprocal(recip_q[g][:], sum_q[g][:])
+                total = stats.tile([P, GB], F32, name="total")
+                nc.vector.tensor_reduce(
+                    total[:], sum_q[g][:].rearrange("p (b i) -> p b i", i=SH), FREE_AXIS, ALU.add
                 )
+                lift[g] = stats.tile([P, GB], F32, name="lift")
+                nc.vector.reciprocal(lift[g][:], total[:])
+                nc.vector.tensor_scalar_mul(lift[g][:], lift[g][:], LIFT)
+
+                weighted[g] = work.tile([P, GB, SH, K], F32, name="weighted")
+                for b in range(GB):
+                    for i in range(SH):
+                        nc.vector.scalar_tensor_tensor(
+                            weighted[g][:, b, i, :],
+                            e[g][:, b, i, :],
+                            recip_q[g][:, b * SH + i : b * SH + i + 1],
+                            e[g][:, b, i, :],
+                            ALU.mult,
+                            ALU.mult,
+                        )
+
+            for g in groups:
+                log_r[g] = work.tile([P, GB, K], F32, name="log_r")
+                for b in range(GB):
+                    nc.scalar.activation(
+                        log_r[g][:, b, :], sum_r[g][:, b, :], ACT.Ln, scale=lift[g][:, b : b + 1]
+                    )
+            for g in groups:
+                recip_lifted[g] = work.tile([P, GB, K], F32, name="recip_lifted")
+                nc.scalar.activation(recip_lifted[g][:], log_r[g][:], ACT.Exp, scale=-1.0)
+
+            for g in groups:
+                sa = work.tile([P, GB, SH, K], F32, name="sa")
+                for b in range(GB):
+                    nc.vector.scalar_tensor_tensor(
+                        sa[:, b, :, :],
+                        weighted[g][:, b, :, :],
+                        lift[g][:, b : b + 1],
+                        recip_lifted[g][:, b, :].unsqueeze(1).to_broadcast([P, SH, K]),
+                        ALU.mult,
+                        ALU.mult,
+                    )
+
+                sa_pairs = sa[:].rearrange("p b (h t) k -> p b h t k", t=2)
+                odd = work.tile([P, GB, 2, K], F32, name="odd")
+                nc.vector.tensor_scalar_add(odd[:], sa_pairs[:, :, :, 1, :], 1.0)
+                halves = work.tile([P, GB, 2, K], F32, name="halves")
+                nc.vector.scalar_tensor_tensor(
+                    halves[:], sa_pairs[:, :, :, 0, :], 1.0, odd[:], ALU.add, ALU.mult
+                )
+
+                at = (g % GROUPS_IN_PIECE) * GB * P
+                for h in range(2):
+                    turned = turned_psum.tile([K, GB * P], F32, name=f"turned{h}")
+                    for b in range(GB):
+                        nc.tensor.transpose(turned[:, b * P : (b + 1) * P], halves[:, b, h, :], ident_f[:])
+                    nc.scalar.copy(factors[piece][h][:, at : at + GB * P], turned[:])
+
+            list_cols = slice(piece * PIECE // 16, (piece + 1) * PIECE // 16)
+            nc.vector.tensor_tensor(
+                window[:].indirect(offsets[:, list_cols]),
+                factors[piece][0][:],
+                factors[piece][1][:],
+                ALU.mult,
+            )
 
         nc.sync.dma_start(out, window[:])

@@ -15,7 +15,6 @@ GB = 4
 GROUPS = N // (GB * P)
 PIECE = 1024
 GROUPS_IN_PIECE = PIECE // (GB * P)
-LIFT = 2.0**32
 
 FLOPS = 2 * K * SH * D * N
 
@@ -24,8 +23,8 @@ def tile_sralnet_kernel(tc, x, centroids, base, offs, out):
     nc = tc.nc
     with (
         tc.tile_pool(name="held", bufs=1) as held,
-        tc.tile_pool(name="work", bufs=4) as work,
-        tc.tile_pool(name="stats", bufs=4) as stats,
+        tc.tile_pool(name="work", bufs=3) as work,
+        tc.tile_pool(name="stats", bufs=3) as stats,
         tc.psum_pool(name="setup_psum", bufs=1) as setup_psum,
         tc.psum_pool(name="z_psum", bufs=3) as z_psum,
         tc.psum_pool(name="turned_psum", bufs=2) as turned_psum,
@@ -83,100 +82,75 @@ def tile_sralnet_kernel(tc, x, centroids, base, offs, out):
             for piece in range(N // PIECE)
         ]
 
-        for piece in range(N // PIECE):
-            groups = range(piece * GROUPS_IN_PIECE, (piece + 1) * GROUPS_IN_PIECE)
-            e, sum_q, sum_r, recip_q, lift, log_r, recip_lifted, weighted = {}, {}, {}, {}, {}, {}, {}, {}
-
-            for g in groups:
-                e[g] = work.tile([P, GB, SH, K], F32, name="e")
-                sum_q[g] = stats.tile([P, GB * SH], F32, name="sum_q")
-                for b in range(GB):
-                    first = (g * GB + b) * P
-                    z = z_psum.tile([P, SH * K], F32, name="z")
-                    nc.tensor.matmul(z[:], pixels[:, first : first + P], cents_t[:], start=True, stop=False)
-                    nc.tensor.matmul(z[:], ones_b[:], rows[:], start=False, stop=True)
-                    for i in range(SH):
-                        nc.scalar.activation(
-                            e[g][:, b, i, :],
-                            z[:, i * K : (i + 1) * K],
-                            ACT.Exp,
-                            scale=2.0 * ALPHA,
-                            accum_out=sum_q[g][:, b * SH + i : b * SH + i + 1],
-                        )
-
-            for g in groups:
-                pair01 = work.tile([P, GB, K], F32, name="pair01")
-                nc.gpsimd.tensor_tensor(pair01[:], e[g][:, :, 0, :], e[g][:, :, 1, :], ALU.add)
-                pair23 = work.tile([P, GB, K], F32, name="pair23")
-                nc.gpsimd.tensor_tensor(pair23[:], e[g][:, :, 2, :], e[g][:, :, 3, :], ALU.add)
-                sum_r[g] = work.tile([P, GB, K], F32, name="sum_r")
-                nc.gpsimd.tensor_tensor(sum_r[g][:], pair01[:], pair23[:], ALU.add)
-
-                recip_q[g] = stats.tile([P, GB * SH], F32, name="recip_q")
-                nc.vector.reciprocal(recip_q[g][:], sum_q[g][:])
-                total = stats.tile([P, GB], F32, name="total")
-                nc.vector.tensor_reduce(
-                    total[:], sum_q[g][:].rearrange("p (b i) -> p b i", i=SH), FREE_AXIS, ALU.add
-                )
-                lift[g] = stats.tile([P, GB], F32, name="lift")
-                nc.vector.reciprocal(lift[g][:], total[:])
-                nc.vector.tensor_scalar_mul(lift[g][:], lift[g][:], LIFT)
-
-                weighted[g] = work.tile([P, GB, SH, K], F32, name="weighted")
-                for b in range(GB):
-                    for i in range(SH):
-                        nc.vector.scalar_tensor_tensor(
-                            weighted[g][:, b, i, :],
-                            e[g][:, b, i, :],
-                            recip_q[g][:, b * SH + i : b * SH + i + 1],
-                            e[g][:, b, i, :],
-                            ALU.mult,
-                            ALU.mult,
-                        )
-
-            for g in groups:
-                log_r[g] = work.tile([P, GB, K], F32, name="log_r")
-                for b in range(GB):
+        for g in range(GROUPS):
+            e = work.tile([P, GB, SH, K], F32, name="e")
+            sum_q = stats.tile([P, GB * SH], F32, name="sum_q")
+            for b in range(GB):
+                first = (g * GB + b) * P
+                z = z_psum.tile([P, SH * K], F32, name="z")
+                nc.tensor.matmul(z[:], pixels[:, first : first + P], cents_t[:], start=True, stop=False)
+                nc.tensor.matmul(z[:], ones_b[:], rows[:], start=False, stop=True)
+                for i in range(SH):
                     nc.scalar.activation(
-                        log_r[g][:, b, :], sum_r[g][:, b, :], ACT.Ln, scale=lift[g][:, b : b + 1]
+                        e[:, b, i, :],
+                        z[:, i * K : (i + 1) * K],
+                        ACT.Exp,
+                        scale=2.0 * ALPHA,
+                        accum_out=sum_q[:, b * SH + i : b * SH + i + 1],
                     )
-            for g in groups:
-                recip_lifted[g] = work.tile([P, GB, K], F32, name="recip_lifted")
-                nc.scalar.activation(recip_lifted[g][:], log_r[g][:], ACT.Exp, scale=-1.0)
 
-            for g in groups:
-                sa = work.tile([P, GB, SH, K], F32, name="sa")
-                for b in range(GB):
+            pair01 = work.tile([P, GB, K], F32, name="pair01")
+            nc.gpsimd.tensor_tensor(pair01[:], e[:, :, 0, :], e[:, :, 1, :], ALU.add)
+            pair23 = work.tile([P, GB, K], F32, name="pair23")
+            nc.gpsimd.tensor_tensor(pair23[:], e[:, :, 2, :], e[:, :, 3, :], ALU.add)
+            sum_r = work.tile([P, GB, K], F32, name="sum_r")
+            nc.gpsimd.tensor_tensor(sum_r[:], pair01[:], pair23[:], ALU.add)
+
+            recip_q = stats.tile([P, GB * SH], F32, name="recip_q")
+            nc.vector.reciprocal(recip_q[:], sum_q[:])
+
+            recip_r = work.tile([P, GB, K], F32, name="recip_r")
+            nc.vector.reciprocal(recip_r[:], sum_r[:])
+
+            weighted = work.tile([P, GB, SH, K], F32, name="weighted")
+            for b in range(GB):
+                for i in range(SH):
                     nc.vector.scalar_tensor_tensor(
-                        sa[:, b, :, :],
-                        weighted[g][:, b, :, :],
-                        lift[g][:, b : b + 1],
-                        recip_lifted[g][:, b, :].unsqueeze(1).to_broadcast([P, SH, K]),
+                        weighted[:, b, i, :],
+                        e[:, b, i, :],
+                        recip_q[:, b * SH + i : b * SH + i + 1],
+                        e[:, b, i, :],
                         ALU.mult,
                         ALU.mult,
                     )
-
-                sa_pairs = sa[:].rearrange("p b (h t) k -> p b h t k", t=2)
-                odd = work.tile([P, GB, 2, K], F32, name="odd")
-                nc.vector.tensor_scalar_add(odd[:], sa_pairs[:, :, :, 1, :], 1.0)
-                halves = work.tile([P, GB, 2, K], F32, name="halves")
-                nc.vector.scalar_tensor_tensor(
-                    halves[:], sa_pairs[:, :, :, 0, :], 1.0, odd[:], ALU.add, ALU.mult
-                )
-
-                at = (g % GROUPS_IN_PIECE) * GB * P
-                for h in range(2):
-                    turned = turned_psum.tile([K, GB * P], F32, name=f"turned{h}")
-                    for b in range(GB):
-                        nc.tensor.transpose(turned[:, b * P : (b + 1) * P], halves[:, b, h, :], ident_f[:])
-                    nc.scalar.copy(factors[piece][h][:, at : at + GB * P], turned[:])
-
-            list_cols = slice(piece * PIECE // 16, (piece + 1) * PIECE // 16)
+            sa = work.tile([P, GB, SH, K], F32, name="sa")
             nc.vector.tensor_tensor(
-                window[:].indirect(offsets[:, list_cols]),
-                factors[piece][0][:],
-                factors[piece][1][:],
-                ALU.mult,
+                sa[:], weighted[:], recip_r[:].unsqueeze(2).to_broadcast([P, GB, SH, K]), ALU.mult
             )
+
+            sa_pairs = sa[:].rearrange("p b (h t) k -> p b h t k", t=2)
+            odd = work.tile([P, GB, 2, K], F32, name="odd")
+            nc.vector.tensor_scalar_add(odd[:], sa_pairs[:, :, :, 1, :], 1.0)
+            halves = work.tile([P, GB, 2, K], F32, name="halves")
+            nc.vector.scalar_tensor_tensor(
+                halves[:], sa_pairs[:, :, :, 0, :], 1.0, odd[:], ALU.add, ALU.mult
+            )
+
+            piece = g // GROUPS_IN_PIECE
+            at = (g % GROUPS_IN_PIECE) * GB * P
+            for h in range(2):
+                turned = turned_psum.tile([K, GB * P], F32, name=f"turned{h}")
+                for b in range(GB):
+                    nc.tensor.transpose(turned[:, b * P : (b + 1) * P], halves[:, b, h, :], ident_f[:])
+                nc.scalar.copy(factors[piece][h][:, at : at + GB * P], turned[:])
+
+            if g % GROUPS_IN_PIECE == GROUPS_IN_PIECE - 1:
+                list_cols = slice(piece * PIECE // 16, (piece + 1) * PIECE // 16)
+                nc.vector.tensor_tensor(
+                    window[:].indirect(offsets[:, list_cols]),
+                    factors[piece][0][:],
+                    factors[piece][1][:],
+                    ALU.mult,
+                )
 
         nc.sync.dma_start(out, window[:])

@@ -15,6 +15,7 @@ GB = 4
 GROUPS = N // (GB * P)
 PIECE = 1024
 GROUPS_IN_PIECE = PIECE // (GB * P)
+LIFT = 2.0**32
 
 FLOPS = 2 * K * SH * D * N
 
@@ -23,11 +24,10 @@ def tile_sralnet_kernel(tc, x, centroids, base, offs, out):
     nc = tc.nc
     with (
         tc.tile_pool(name="held", bufs=1) as held,
-        tc.tile_pool(name="work", bufs=3) as work,
-        tc.tile_pool(name="stats", bufs=3) as stats,
-        tc.psum_pool(name="setup_psum", bufs=1) as setup_psum,
-        tc.psum_pool(name="z_psum", bufs=3) as z_psum,
-        tc.psum_pool(name="turned_psum", bufs=2) as turned_psum,
+        tc.tile_pool(name="work", bufs=4) as work,
+        tc.tile_pool(name="stats", bufs=4) as stats,
+        tc.psum_pool(name="z_psum", bufs=4) as z_psum,
+        tc.psum_pool(name="turned_psum", bufs=1) as turned_psum,
     ):
         offsets = held.tile([P, N // 16], U16, name="offsets")
         nc.sync.dma_start(offsets[:], offs)
@@ -49,7 +49,7 @@ def tile_sralnet_kernel(tc, x, centroids, base, offs, out):
         half = held.tile([K, SH], F32, name="half")
         nc.vector.memset(half[:], 0.5)
 
-        cents_t_ps = setup_psum.tile([D, SH * K], BF16, name="cents_t_ps", tag="setup")
+        cents_t_ps = z_psum.tile([D, SH * K], BF16, name="cents_t_ps", tag="z")
         for i in range(SH):
             nc.tensor.transpose(cents_t_ps[:, i * K : (i + 1) * K], cents[:, i, :], ident_b[:])
         cents_t = held.tile([D, SH * K], BF16, name="cents_t")
@@ -71,7 +71,7 @@ def tile_sralnet_kernel(tc, x, centroids, base, offs, out):
         nc.vector.tensor_tensor(rest[:], shift[:], pieces[:, :, 0], ALU.subtract)
         nc.vector.tensor_copy(pieces[:, :, 1], rest[:])
         nc.vector.tensor_tensor(pieces[:, :, 2], rest[:], pieces[:, :, 1], ALU.subtract)
-        rows_ps = setup_psum.tile([P, SH * K], BF16, name="rows_ps", tag="setup")
+        rows_ps = z_psum.tile([P, SH * K], BF16, name="rows_ps", tag="z")
         for i in range(SH):
             nc.tensor.transpose(rows_ps[:, i * K : (i + 1) * K], pieces[:, i, :], ident_b[:])
         rows = held.tile([P, SH * K], BF16, name="rows")
@@ -82,75 +82,98 @@ def tile_sralnet_kernel(tc, x, centroids, base, offs, out):
             for piece in range(N // PIECE)
         ]
 
-        for g in range(GROUPS):
-            e = work.tile([P, GB, SH, K], F32, name="e")
-            sum_q = stats.tile([P, GB * SH], F32, name="sum_q")
-            for b in range(GB):
-                first = (g * GB + b) * P
-                z = z_psum.tile([P, SH * K], F32, name="z")
-                nc.tensor.matmul(z[:], pixels[:, first : first + P], cents_t[:], start=True, stop=False)
-                nc.tensor.matmul(z[:], ones_b[:], rows[:], start=False, stop=True)
-                for i in range(SH):
-                    nc.scalar.activation(
-                        e[:, b, i, :],
-                        z[:, i * K : (i + 1) * K],
-                        ACT.Exp,
-                        scale=2.0 * ALPHA,
-                        accum_out=sum_q[:, b * SH + i : b * SH + i + 1],
-                    )
+        for piece in range(N // PIECE):
+            groups = range(piece * GROUPS_IN_PIECE, (piece + 1) * GROUPS_IN_PIECE)
+            e, sum_q, sum_r, recip_q, lift, log_r, recip_lifted, weighted = {}, {}, {}, {}, {}, {}, {}, {}
 
-            pair01 = work.tile([P, GB, K], F32, name="pair01")
-            nc.gpsimd.tensor_tensor(pair01[:], e[:, :, 0, :], e[:, :, 1, :], ALU.add)
-            pair23 = work.tile([P, GB, K], F32, name="pair23")
-            nc.gpsimd.tensor_tensor(pair23[:], e[:, :, 2, :], e[:, :, 3, :], ALU.add)
-            sum_r = work.tile([P, GB, K], F32, name="sum_r")
-            nc.gpsimd.tensor_tensor(sum_r[:], pair01[:], pair23[:], ALU.add)
-
-            recip_q = stats.tile([P, GB * SH], F32, name="recip_q")
-            nc.vector.reciprocal(recip_q[:], sum_q[:])
-
-            recip_r = work.tile([P, GB, K], F32, name="recip_r")
-            nc.vector.reciprocal(recip_r[:], sum_r[:])
-
-            weighted = work.tile([P, GB, SH, K], F32, name="weighted")
-            for b in range(GB):
-                for i in range(SH):
-                    nc.vector.scalar_tensor_tensor(
-                        weighted[:, b, i, :],
-                        e[:, b, i, :],
-                        recip_q[:, b * SH + i : b * SH + i + 1],
-                        e[:, b, i, :],
-                        ALU.mult,
-                        ALU.mult,
-                    )
-            sa = work.tile([P, GB, SH, K], F32, name="sa")
-            nc.vector.tensor_tensor(
-                sa[:], weighted[:], recip_r[:].unsqueeze(2).to_broadcast([P, GB, SH, K]), ALU.mult
-            )
-
-            sa_pairs = sa[:].rearrange("p b (h t) k -> p b h t k", t=2)
-            odd = work.tile([P, GB, 2, K], F32, name="odd")
-            nc.vector.tensor_scalar_add(odd[:], sa_pairs[:, :, :, 1, :], 1.0)
-            halves = work.tile([P, GB, 2, K], F32, name="halves")
-            nc.vector.scalar_tensor_tensor(
-                halves[:], sa_pairs[:, :, :, 0, :], 1.0, odd[:], ALU.add, ALU.mult
-            )
-
-            piece = g // GROUPS_IN_PIECE
-            at = (g % GROUPS_IN_PIECE) * GB * P
-            for h in range(2):
-                turned = turned_psum.tile([K, GB * P], F32, name=f"turned{h}")
+            for g in groups:
+                e[g] = work.tile([P, GB, SH, K], F32, name="e")
+                sum_q[g] = stats.tile([P, GB * SH], F32, name="sum_q")
                 for b in range(GB):
-                    nc.tensor.transpose(turned[:, b * P : (b + 1) * P], halves[:, b, h, :], ident_f[:])
-                nc.scalar.copy(factors[piece][h][:, at : at + GB * P], turned[:])
+                    first = (g * GB + b) * P
+                    z = z_psum.tile([P, SH * K], F32, name="z")
+                    nc.tensor.matmul(z[:], pixels[:, first : first + P], cents_t[:], start=True, stop=False)
+                    nc.tensor.matmul(z[:], ones_b[:], rows[:], start=False, stop=True)
+                    for i in range(SH):
+                        nc.scalar.activation(
+                            e[g][:, b, i, :],
+                            z[:, i * K : (i + 1) * K],
+                            ACT.Exp,
+                            scale=2.0 * ALPHA,
+                            accum_out=sum_q[g][:, b * SH + i : b * SH + i + 1],
+                        )
 
-            if g % GROUPS_IN_PIECE == GROUPS_IN_PIECE - 1:
-                list_cols = slice(piece * PIECE // 16, (piece + 1) * PIECE // 16)
-                nc.vector.tensor_tensor(
-                    window[:].indirect(offsets[:, list_cols]),
-                    factors[piece][0][:],
-                    factors[piece][1][:],
-                    ALU.mult,
+            for g in groups:
+                pair01 = work.tile([P, GB, K], F32, name="pair01")
+                nc.gpsimd.tensor_tensor(pair01[:], e[g][:, :, 0, :], e[g][:, :, 1, :], ALU.add)
+                pair23 = work.tile([P, GB, K], F32, name="pair23")
+                nc.gpsimd.tensor_tensor(pair23[:], e[g][:, :, 2, :], e[g][:, :, 3, :], ALU.add)
+                sum_r[g] = work.tile([P, GB, K], F32, name="sum_r")
+                nc.gpsimd.tensor_tensor(sum_r[g][:], pair01[:], pair23[:], ALU.add)
+
+                recip_q[g] = stats.tile([P, GB * SH], F32, name="recip_q")
+                nc.vector.reciprocal(recip_q[g][:], sum_q[g][:])
+                total = stats.tile([P, GB], F32, name="total")
+                nc.vector.tensor_reduce(
+                    total[:], sum_q[g][:].rearrange("p (b i) -> p b i", i=SH), FREE_AXIS, ALU.add
                 )
+                lift[g] = stats.tile([P, GB], F32, name="lift")
+                nc.vector.reciprocal(lift[g][:], total[:])
+                nc.vector.tensor_scalar_mul(lift[g][:], lift[g][:], LIFT)
+
+                weighted[g] = work.tile([P, GB, SH, K], F32, name="weighted")
+                for b in range(GB):
+                    for i in range(SH):
+                        nc.vector.scalar_tensor_tensor(
+                            weighted[g][:, b, i, :],
+                            e[g][:, b, i, :],
+                            recip_q[g][:, b * SH + i : b * SH + i + 1],
+                            e[g][:, b, i, :],
+                            ALU.mult,
+                            ALU.mult,
+                        )
+
+            for g in groups:
+                log_r[g] = work.tile([P, GB, K], F32, name="log_r")
+                for b in range(GB):
+                    nc.scalar.activation(
+                        log_r[g][:, b, :], sum_r[g][:, b, :], ACT.Ln, scale=lift[g][:, b : b + 1]
+                    )
+            for g in groups:
+                recip_lifted[g] = work.tile([P, GB, K], F32, name="recip_lifted")
+                nc.scalar.activation(recip_lifted[g][:], log_r[g][:], ACT.Exp, scale=-1.0)
+
+            for g in groups:
+                sa = work.tile([P, GB, SH, K], F32, name="sa")
+                for b in range(GB):
+                    nc.vector.scalar_tensor_tensor(
+                        sa[:, b, :, :],
+                        weighted[g][:, b, :, :],
+                        lift[g][:, b : b + 1],
+                        recip_lifted[g][:, b, :].unsqueeze(1).to_broadcast([P, SH, K]),
+                        ALU.mult,
+                        ALU.mult,
+                    )
+
+                turned = [turned_psum.tile([K, GB * P], F32, name=f"turned{i}") for i in range(SH)]
+                for i in range(SH):
+                    for b in range(GB):
+                        nc.tensor.transpose(turned[i][:, b * P : (b + 1) * P], sa[:, b, i, :], ident_f[:])
+
+                at = (g % GROUPS_IN_PIECE) * GB * P
+                for h in range(2):
+                    odd = work.tile([K, GB * P], F32, name="odd")
+                    nc.vector.tensor_scalar_add(odd[:], turned[2 * h + 1][:], 1.0)
+                    nc.vector.scalar_tensor_tensor(
+                        factors[piece][h][:, at : at + GB * P], turned[2 * h][:], 1.0, odd[:], ALU.add, ALU.mult
+                    )
+
+            list_cols = slice(piece * PIECE // 16, (piece + 1) * PIECE // 16)
+            nc.vector.tensor_tensor(
+                window[:].indirect(offsets[:, list_cols]),
+                factors[piece][0][:],
+                factors[piece][1][:],
+                ALU.mult,
+            )
 
         nc.sync.dma_start(out, window[:])

@@ -1,3 +1,5 @@
+import math
+
 import concourse.mybir as mybir
 from concourse.masks import make_identity
 
@@ -12,9 +14,8 @@ K, SH, D, S, N = 128, 4, 128, 4096, 2048
 ALPHA = 100.0
 P = 128
 GB = 4
-GROUPS = N // (GB * P)
-PIECE = 1024
-GROUPS_IN_PIECE = PIECE // (GB * P)
+GROUP = GB * P
+GROUPS = N // GROUP
 LIFT = 2.0**32
 
 FLOPS = 2 * K * SH * D * N
@@ -24,10 +25,11 @@ def tile_sralnet_kernel(tc, x, centroids, base, offs, out):
     nc = tc.nc
     with (
         tc.tile_pool(name="held", bufs=1) as held,
-        tc.tile_pool(name="work", bufs=4) as work,
-        tc.tile_pool(name="stats", bufs=4) as stats,
-        tc.psum_pool(name="z_psum", bufs=4) as z_psum,
-        tc.psum_pool(name="turned_psum", bufs=1) as turned_psum,
+        tc.tile_pool(name="work", bufs=GROUPS) as work,
+        tc.tile_pool(name="stats", bufs=GROUPS) as stats,
+        tc.tile_pool(name="last", bufs=2) as last,
+        tc.psum_pool(name="z_psum", bufs=3) as z_psum,
+        tc.psum_pool(name="zc_psum", bufs=4) as zc_psum,
     ):
         offsets = held.tile([P, N // 16], U16, name="offsets")
         nc.sync.dma_start(offsets[:], offs)
@@ -35,7 +37,7 @@ def tile_sralnet_kernel(tc, x, centroids, base, offs, out):
         nc.sync.dma_start(cents[:], centroids)
         pixels = held.tile([D, N], BF16, name="pixels")
         for g in range(GROUPS):
-            cols = slice(g * GB * P, (g + 1) * GB * P)
+            cols = slice(g * GROUP, (g + 1) * GROUP)
             nc.sync.dma_start(pixels[:, cols], x[:, cols])
         window = held.tile([K, S], F32, name="window")
         nc.sync.dma_start(window[:], base)
@@ -46,7 +48,7 @@ def tile_sralnet_kernel(tc, x, centroids, base, offs, out):
         nc.vector.tensor_copy(ident_b[:], ident_f[:])
         ones_b = held.tile([P, P], BF16, name="ones_b")
         nc.vector.memset(ones_b[:], 1.0)
-        half = held.tile([K, SH], F32, name="half")
+        half = held.tile([P, SH], F32, name="half")
         nc.vector.memset(half[:], 0.5)
 
         cents_t_ps = z_psum.tile([D, SH * K], BF16, name="cents_t_ps", tag="z")
@@ -63,6 +65,8 @@ def tile_sralnet_kernel(tc, x, centroids, base, offs, out):
         nc.gpsimd.tensor_tensor(norm[:], sumsq[:], half[:], ALU.pow)
         shift = held.tile([K, SH], F32, name="shift")
         nc.vector.tensor_scalar_mul(shift[:], norm[:], -0.5)
+        twice_bias = held.tile([K, SH], F32, name="twice_bias")
+        nc.vector.tensor_scalar_mul(twice_bias[:], norm[:], -2.0 * ALPHA)
 
         pieces = held.tile([K, SH, P], BF16, name="pieces")
         nc.vector.memset(pieces[:], 0.0)
@@ -77,103 +81,103 @@ def tile_sralnet_kernel(tc, x, centroids, base, offs, out):
         rows = held.tile([P, SH * K], BF16, name="rows")
         nc.vector.tensor_copy(rows[:], rows_ps[:])
 
-        factors = [
-            [held.tile([K, PIECE], F32, name=f"factor{piece}{h}") for h in range(2)]
-            for piece in range(N // PIECE)
-        ]
+        sum_r, lift, q_lifted, root_total = {}, {}, {}, {}
+        log_r, log_q, log_root = {}, {}, {}
 
-        for piece in range(N // PIECE):
-            groups = range(piece * GROUPS_IN_PIECE, (piece + 1) * GROUPS_IN_PIECE)
-            e, sum_q, sum_r, recip_q, lift, log_r, recip_lifted, weighted = {}, {}, {}, {}, {}, {}, {}, {}
-
-            for g in groups:
-                e[g] = work.tile([P, GB, SH, K], F32, name="e")
-                sum_q[g] = stats.tile([P, GB * SH], F32, name="sum_q")
-                for b in range(GB):
-                    first = (g * GB + b) * P
-                    z = z_psum.tile([P, SH * K], F32, name="z")
-                    nc.tensor.matmul(z[:], pixels[:, first : first + P], cents_t[:], start=True, stop=False)
-                    nc.tensor.matmul(z[:], ones_b[:], rows[:], start=False, stop=True)
-                    for i in range(SH):
-                        nc.scalar.activation(
-                            e[g][:, b, i, :],
-                            z[:, i * K : (i + 1) * K],
-                            ACT.Exp,
-                            scale=2.0 * ALPHA,
-                            accum_out=sum_q[g][:, b * SH + i : b * SH + i + 1],
-                        )
-
-            for g in groups:
-                pair01 = work.tile([P, GB, K], F32, name="pair01")
-                nc.gpsimd.tensor_tensor(pair01[:], e[g][:, :, 0, :], e[g][:, :, 1, :], ALU.add)
-                pair23 = work.tile([P, GB, K], F32, name="pair23")
-                nc.gpsimd.tensor_tensor(pair23[:], e[g][:, :, 2, :], e[g][:, :, 3, :], ALU.add)
-                sum_r[g] = work.tile([P, GB, K], F32, name="sum_r")
-                nc.gpsimd.tensor_tensor(sum_r[g][:], pair01[:], pair23[:], ALU.add)
-
-                recip_q[g] = stats.tile([P, GB * SH], F32, name="recip_q")
-                nc.vector.reciprocal(recip_q[g][:], sum_q[g][:])
-                total = stats.tile([P, GB], F32, name="total")
-                nc.vector.tensor_reduce(
-                    total[:], sum_q[g][:].rearrange("p (b i) -> p b i", i=SH), FREE_AXIS, ALU.add
-                )
-                lift[g] = stats.tile([P, GB], F32, name="lift")
-                nc.vector.reciprocal(lift[g][:], total[:])
-                nc.vector.tensor_scalar_mul(lift[g][:], lift[g][:], LIFT)
-
-                weighted[g] = work.tile([P, GB, SH, K], F32, name="weighted")
-                for b in range(GB):
-                    for i in range(SH):
-                        nc.vector.scalar_tensor_tensor(
-                            weighted[g][:, b, i, :],
-                            e[g][:, b, i, :],
-                            recip_q[g][:, b * SH + i : b * SH + i + 1],
-                            e[g][:, b, i, :],
-                            ALU.mult,
-                            ALU.mult,
-                        )
-
-            for g in groups:
-                log_r[g] = work.tile([P, GB, K], F32, name="log_r")
-                for b in range(GB):
-                    nc.scalar.activation(
-                        log_r[g][:, b, :], sum_r[g][:, b, :], ACT.Ln, scale=lift[g][:, b : b + 1]
-                    )
-            for g in groups:
-                recip_lifted[g] = work.tile([P, GB, K], F32, name="recip_lifted")
-                nc.scalar.activation(recip_lifted[g][:], log_r[g][:], ACT.Exp, scale=-1.0)
-
-            for g in groups:
-                sa = work.tile([P, GB, SH, K], F32, name="sa")
-                for b in range(GB):
-                    nc.vector.scalar_tensor_tensor(
-                        sa[:, b, :, :],
-                        weighted[g][:, b, :, :],
-                        lift[g][:, b : b + 1],
-                        recip_lifted[g][:, b, :].unsqueeze(1).to_broadcast([P, SH, K]),
-                        ALU.mult,
-                        ALU.mult,
-                    )
-
-                turned = [turned_psum.tile([K, GB * P], F32, name=f"turned{i}") for i in range(SH)]
+        for g in range(GROUPS):
+            e = work.tile([P, GB, SH, K], F32, name="e")
+            sum_q = stats.tile([P, GB, SH], F32, name="sum_q")
+            for b in range(GB):
+                first = (g * GB + b) * P
+                z = z_psum.tile([P, SH * K], F32, name="z")
+                nc.tensor.matmul(z[:], pixels[:, first : first + P], cents_t[:], start=True, stop=False)
+                nc.tensor.matmul(z[:], ones_b[:], rows[:], start=False, stop=True)
                 for i in range(SH):
-                    for b in range(GB):
-                        nc.tensor.transpose(turned[i][:, b * P : (b + 1) * P], sa[:, b, i, :], ident_f[:])
-
-                at = (g % GROUPS_IN_PIECE) * GB * P
-                for h in range(2):
-                    odd = work.tile([K, GB * P], F32, name="odd")
-                    nc.vector.tensor_scalar_add(odd[:], turned[2 * h + 1][:], 1.0)
-                    nc.vector.scalar_tensor_tensor(
-                        factors[piece][h][:, at : at + GB * P], turned[2 * h][:], 1.0, odd[:], ALU.add, ALU.mult
+                    nc.scalar.activation(
+                        e[:, b, i, :],
+                        z[:, i * K : (i + 1) * K],
+                        ACT.Exp,
+                        scale=2.0 * ALPHA,
+                        accum_out=sum_q[:, b, i : i + 1],
                     )
 
-            list_cols = slice(piece * PIECE // 16, (piece + 1) * PIECE // 16)
+            pair01 = work.tile([P, GB, K], F32, name="pair01")
+            nc.vector.tensor_tensor(pair01[:], e[:, :, 0, :], e[:, :, 1, :], ALU.add)
+            pair23 = work.tile([P, GB, K], F32, name="pair23")
+            nc.vector.tensor_tensor(pair23[:], e[:, :, 2, :], e[:, :, 3, :], ALU.add)
+            sum_r[g] = work.tile([P, GB, K], F32, name="sum_r")
+            nc.vector.tensor_tensor(sum_r[g][:], pair01[:], pair23[:], ALU.add)
+
+            total = stats.tile([P, GB], F32, name="total")
+            nc.vector.tensor_reduce(total[:], sum_q[:], FREE_AXIS, ALU.add)
+            lift[g] = stats.tile([P, GB], F32, name="lift")
+            nc.vector.reciprocal(lift[g][:], total[:])
+            nc.vector.tensor_scalar_mul(lift[g][:], lift[g][:], LIFT)
+            q_lifted[g] = stats.tile([P, GB, SH], F32, name="q_lifted")
             nc.vector.tensor_tensor(
-                window[:].indirect(offsets[:, list_cols]),
-                factors[piece][0][:],
-                factors[piece][1][:],
+                q_lifted[g][:], sum_q[:], lift[g][:].unsqueeze(2).to_broadcast([P, GB, SH]), ALU.mult
+            )
+            root_total[g] = stats.tile([P, GB], F32, name="root_total")
+            nc.gpsimd.tensor_tensor(root_total[g][:], total[:], half[:, :GB], ALU.pow)
+
+        for g in range(GROUPS):
+            log_r[g] = work.tile([P, GB, K], F32, name="log_r")
+            for b in range(GB):
+                nc.scalar.activation(log_r[g][:, b, :], sum_r[g][:, b, :], ACT.Ln, scale=lift[g][:, b : b + 1])
+            log_q[g] = stats.tile([P, GB, SH], F32, name="log_q")
+            nc.scalar.activation(log_q[g][:], q_lifted[g][:], ACT.Ln)
+            log_root[g] = stats.tile([P, GB], F32, name="log_root")
+            nc.scalar.activation(log_root[g][:], root_total[g][:], ACT.Ln)
+
+        for g in range(GROUPS):
+            minus_r = work.tile([P, GB, K], F32, name="minus_r")
+            nc.vector.tensor_scalar_mul(minus_r[:], log_r[g][:], -1.0 / (4.0 * ALPHA))
+            unlift = stats.tile([P, GB], F32, name="unlift")
+            nc.vector.tensor_scalar(
+                unlift[:], log_root[g][:], -4.0 / (4.0 * ALPHA), 64.0 * math.log(2.0) / (4.0 * ALPHA), ALU.mult, ALU.add
+            )
+            minus_q = stats.tile([P, GB, SH], F32, name="minus_q")
+            nc.vector.scalar_tensor_tensor(
+                minus_q[:],
+                log_q[g][:],
+                -1.0 / (4.0 * ALPHA),
+                unlift[:].unsqueeze(2).to_broadcast([P, GB, SH]),
                 ALU.mult,
+                ALU.add,
+            )
+
+            sa = last.tile([K, SH, GROUP], F32, name="sa")
+            for i in range(SH):
+                zc = zc_psum.tile([K, GROUP], F32, name="zc")
+                nc.tensor.matmul(
+                    zc[:], cents_t[:, i * K : (i + 1) * K], pixels[:, g * GROUP : (g + 1) * GROUP], start=True, stop=False
+                )
+                for b in range(GB):
+                    cols = slice(b * P, (b + 1) * P)
+                    nc.tensor.matmul(
+                        zc[:, cols], minus_r[:, b, :], ident_f[:], is_transpose=True, start=False, stop=False
+                    )
+                    nc.tensor.matmul(
+                        zc[:, cols],
+                        minus_q[:, b, i : i + 1].to_broadcast([P, K]),
+                        ident_f[:],
+                        is_transpose=True,
+                        start=False,
+                        stop=(b == GB - 1),
+                    )
+                nc.scalar.activation(sa[:, i, :], zc[:], ACT.Exp, scale=4.0 * ALPHA, bias=twice_bias[:, i : i + 1])
+
+            factors = []
+            for h in range(2):
+                odd = last.tile([K, GROUP], F32, name="odd")
+                nc.vector.tensor_scalar_add(odd[:], sa[:, 2 * h + 1, :], 1.0)
+                factor = last.tile([K, GROUP], F32, name=f"factor{h}")
+                nc.vector.scalar_tensor_tensor(factor[:], sa[:, 2 * h, :], 1.0, odd[:], ALU.add, ALU.mult)
+                factors.append(factor)
+
+            list_cols = slice(g * GROUP // 16, (g + 1) * GROUP // 16)
+            nc.vector.tensor_tensor(
+                window[:].indirect(offsets[:, list_cols]), factors[0][:], factors[1][:], ALU.mult
             )
 
         nc.sync.dma_start(out, window[:])

@@ -26,19 +26,19 @@ def tile_sralnet_kernel(tc, x, centroids, base, offs, out):
     with (
         tc.tile_pool(name="held", bufs=1) as held,
         tc.tile_pool(name="work", bufs=GROUPS) as work,
-        tc.tile_pool(name="stats", bufs=GROUPS) as stats,
         tc.tile_pool(name="last", bufs=2) as last,
-        tc.psum_pool(name="z_psum", bufs=3) as z_psum,
-        tc.psum_pool(name="zc_psum", bufs=4) as zc_psum,
+        tc.psum_pool(name="zc_psum", bufs=3) as zc_psum,
+        tc.psum_pool(name="r_psum", bufs=GROUPS) as r_psum,
+        tc.psum_pool(name="q_psum", bufs=1) as q_psum,
     ):
-        offsets = held.tile([P, N // 16], U16, name="offsets")
-        nc.sync.dma_start(offsets[:], offs)
         cents = held.tile([K, SH, D], BF16, name="cents")
         nc.sync.dma_start(cents[:], centroids)
         pixels = held.tile([D, N], BF16, name="pixels")
         for g in range(GROUPS):
             cols = slice(g * GROUP, (g + 1) * GROUP)
             nc.sync.dma_start(pixels[:, cols], x[:, cols])
+        offsets = held.tile([P, N // 16], U16, name="offsets")
+        nc.sync.dma_start(offsets[:], offs)
         window = held.tile([K, S], F32, name="window")
         nc.sync.dma_start(window[:], base)
 
@@ -46,112 +46,116 @@ def tile_sralnet_kernel(tc, x, centroids, base, offs, out):
         make_identity(nc, ident_f[:])
         ident_b = held.tile([P, P], BF16, name="ident_b")
         nc.vector.tensor_copy(ident_b[:], ident_f[:])
-        ones_b = held.tile([P, P], BF16, name="ones_b")
-        nc.vector.memset(ones_b[:], 1.0)
-        half = held.tile([P, SH], F32, name="half")
+        ones_col = held.tile([K, 1], BF16, name="ones_col")
+        nc.vector.memset(ones_col[:], 1.0)
+        half = held.tile([P, GROUPS, GB], F32, name="half")
         nc.vector.memset(half[:], 0.5)
 
-        cents_t_ps = z_psum.tile([D, SH * K], BF16, name="cents_t_ps", tag="z")
+        cents_t_ps = zc_psum.tile([D, SH * K], BF16, name="cents_t_ps", tag="zc")
         for i in range(SH):
             nc.tensor.transpose(cents_t_ps[:, i * K : (i + 1) * K], cents[:, i, :], ident_b[:])
         cents_t = held.tile([D, SH * K], BF16, name="cents_t")
         nc.vector.tensor_copy(cents_t[:], cents_t_ps[:])
 
-        squares = held.tile([K, SH, D], F32, name="squares")
-        nc.vector.tensor_tensor(squares[:], cents[:], cents[:], ALU.mult)
         sumsq = held.tile([K, SH], F32, name="sumsq")
-        nc.vector.tensor_reduce(sumsq[:], squares[:], FREE_AXIS, ALU.add)
+        for i in range(SH):
+            squares = work.tile([K, D], F32, name="squares")
+            nc.scalar.activation(squares[:], cents[:, i, :], ACT.Square, accum_out=sumsq[:, i : i + 1])
         norm = held.tile([K, SH], F32, name="norm")
-        nc.gpsimd.tensor_tensor(norm[:], sumsq[:], half[:], ALU.pow)
-        shift = held.tile([K, SH], F32, name="shift")
-        nc.vector.tensor_scalar_mul(shift[:], norm[:], -0.5)
+        nc.gpsimd.tensor_tensor(norm[:], sumsq[:], half[:, 0, :SH], ALU.pow)
+        bias = held.tile([K, SH], F32, name="bias")
+        nc.vector.tensor_scalar_mul(bias[:], norm[:], -ALPHA)
         twice_bias = held.tile([K, SH], F32, name="twice_bias")
         nc.vector.tensor_scalar_mul(twice_bias[:], norm[:], -2.0 * ALPHA)
 
-        pieces = held.tile([K, SH, P], BF16, name="pieces")
-        nc.vector.memset(pieces[:], 0.0)
-        rest = held.tile([K, SH], F32, name="rest")
-        nc.vector.tensor_copy(pieces[:, :, 0], shift[:])
-        nc.vector.tensor_tensor(rest[:], shift[:], pieces[:, :, 0], ALU.subtract)
-        nc.vector.tensor_copy(pieces[:, :, 1], rest[:])
-        nc.vector.tensor_tensor(pieces[:, :, 2], rest[:], pieces[:, :, 1], ALU.subtract)
-        rows_ps = z_psum.tile([P, SH * K], BF16, name="rows_ps", tag="z")
-        for i in range(SH):
-            nc.tensor.transpose(rows_ps[:, i * K : (i + 1) * K], pieces[:, i, :], ident_b[:])
-        rows = held.tile([P, SH * K], BF16, name="rows")
-        nc.vector.tensor_copy(rows[:], rows_ps[:])
+        def dot_products(g, i, stop):
+            zc = zc_psum.tile([K, GROUP], F32, name="zc")
+            nc.tensor.matmul(
+                zc[:], cents_t[:, i * K : (i + 1) * K], pixels[:, g * GROUP : (g + 1) * GROUP], start=True, stop=stop
+            )
+            return zc
 
-        sum_r, lift, q_lifted, root_total = {}, {}, {}, {}
-        log_r, log_q, log_root = {}, {}, {}
+        e, e_rounded, sum_r, log_r = {}, {}, {}, {}
+        sum_q = q_psum.tile([P, GROUPS, GB, SH], F32, name="sum_q")
 
-        for g in range(GROUPS):
-            e = work.tile([P, GB, SH, K], F32, name="e")
-            sum_q = stats.tile([P, GB, SH], F32, name="sum_q")
+        def exponentials(g):
+            e[g] = work.tile([K, SH, GROUP], F32, name="e")
+            e_rounded[g] = work.tile([K, SH, GROUP], BF16, name="e_rounded")
+            for i in range(SH):
+                zc = dot_products(g, i, stop=True)
+                nc.scalar.activation(e[g][:, i, :], zc[:], ACT.Exp, scale=2.0 * ALPHA, bias=bias[:, i : i + 1])
+                nc.vector.tensor_copy(e_rounded[g][:, i, :], e[g][:, i, :])
+
+        def sums(g):
             for b in range(GB):
-                first = (g * GB + b) * P
-                z = z_psum.tile([P, SH * K], F32, name="z")
-                nc.tensor.matmul(z[:], pixels[:, first : first + P], cents_t[:], start=True, stop=False)
-                nc.tensor.matmul(z[:], ones_b[:], rows[:], start=False, stop=True)
                 for i in range(SH):
-                    nc.scalar.activation(
-                        e[:, b, i, :],
-                        z[:, i * K : (i + 1) * K],
-                        ACT.Exp,
-                        scale=2.0 * ALPHA,
-                        accum_out=sum_q[:, b, i : i + 1],
+                    nc.tensor.matmul(
+                        sum_q[:, g, b, i : i + 1],
+                        e_rounded[g][:, i, b * P : (b + 1) * P],
+                        ones_col[:],
+                        start=True,
+                        stop=True,
+                    )
+            sum_r[g] = r_psum.tile([P, GB, K], F32, name="sum_r")
+            for b in range(GB):
+                for i in range(SH):
+                    nc.tensor.matmul(
+                        sum_r[g][:, b, :],
+                        e[g][:, i, b * P : (b + 1) * P],
+                        ident_f[:],
+                        is_transpose=True,
+                        start=(i == 0),
+                        stop=(i == SH - 1),
                     )
 
-            pair01 = work.tile([P, GB, K], F32, name="pair01")
-            nc.vector.tensor_tensor(pair01[:], e[:, :, 0, :], e[:, :, 1, :], ALU.add)
-            pair23 = work.tile([P, GB, K], F32, name="pair23")
-            nc.vector.tensor_tensor(pair23[:], e[:, :, 2, :], e[:, :, 3, :], ALU.add)
-            sum_r[g] = work.tile([P, GB, K], F32, name="sum_r")
-            nc.vector.tensor_tensor(sum_r[g][:], pair01[:], pair23[:], ALU.add)
+        exponentials(0)
+        for g in range(1, GROUPS):
+            exponentials(g)
+            sums(g - 1)
+        sums(GROUPS - 1)
 
-            total = stats.tile([P, GB], F32, name="total")
-            nc.vector.tensor_reduce(total[:], sum_q[:], FREE_AXIS, ALU.add)
-            lift[g] = stats.tile([P, GB], F32, name="lift")
-            nc.vector.reciprocal(lift[g][:], total[:])
-            nc.vector.tensor_scalar_mul(lift[g][:], lift[g][:], LIFT)
-            q_lifted[g] = stats.tile([P, GB, SH], F32, name="q_lifted")
-            nc.vector.tensor_tensor(
-                q_lifted[g][:], sum_q[:], lift[g][:].unsqueeze(2).to_broadcast([P, GB, SH]), ALU.mult
-            )
-            root_total[g] = stats.tile([P, GB], F32, name="root_total")
-            nc.gpsimd.tensor_tensor(root_total[g][:], total[:], half[:, :GB], ALU.pow)
+        total = held.tile([P, GROUPS, GB], F32, name="total")
+        nc.vector.tensor_reduce(total[:], sum_q[:], FREE_AXIS, ALU.add)
+        lift = held.tile([P, GROUPS, GB], F32, name="lift")
+        nc.vector.reciprocal(lift[:], total[:])
+        nc.vector.tensor_scalar_mul(lift[:], lift[:], LIFT)
+        q_lifted = held.tile([P, GROUPS, GB, SH], F32, name="q_lifted")
+        nc.vector.tensor_tensor(
+            q_lifted[:], sum_q[:], lift[:].unsqueeze(3).to_broadcast([P, GROUPS, GB, SH]), ALU.mult
+        )
+        root_total = held.tile([P, GROUPS, GB], F32, name="root_total")
+        nc.gpsimd.tensor_tensor(root_total[:], total[:], half[:], ALU.pow)
 
         for g in range(GROUPS):
             log_r[g] = work.tile([P, GB, K], F32, name="log_r")
             for b in range(GB):
-                nc.scalar.activation(log_r[g][:, b, :], sum_r[g][:, b, :], ACT.Ln, scale=lift[g][:, b : b + 1])
-            log_q[g] = stats.tile([P, GB, SH], F32, name="log_q")
-            nc.scalar.activation(log_q[g][:], q_lifted[g][:], ACT.Ln)
-            log_root[g] = stats.tile([P, GB], F32, name="log_root")
-            nc.scalar.activation(log_root[g][:], root_total[g][:], ACT.Ln)
+                nc.scalar.activation(log_r[g][:, b, :], sum_r[g][:, b, :], ACT.Ln, scale=lift[:, g, b : b + 1])
+        log_q = held.tile([P, GROUPS, GB, SH], F32, name="log_q")
+        nc.scalar.activation(log_q[:], q_lifted[:], ACT.Ln)
+        log_root = held.tile([P, GROUPS, GB], F32, name="log_root")
+        nc.scalar.activation(log_root[:], root_total[:], ACT.Ln)
+
+        unlift = held.tile([P, GROUPS, GB], F32, name="unlift")
+        nc.vector.tensor_scalar(
+            unlift[:], log_root[:], -4.0 / (4.0 * ALPHA), 64.0 * math.log(2.0) / (4.0 * ALPHA), ALU.mult, ALU.add
+        )
+        minus_q = held.tile([P, GROUPS, GB, SH], F32, name="minus_q")
+        nc.vector.scalar_tensor_tensor(
+            minus_q[:],
+            log_q[:],
+            -1.0 / (4.0 * ALPHA),
+            unlift[:].unsqueeze(3).to_broadcast([P, GROUPS, GB, SH]),
+            ALU.mult,
+            ALU.add,
+        )
 
         for g in range(GROUPS):
             minus_r = work.tile([P, GB, K], F32, name="minus_r")
             nc.vector.tensor_scalar_mul(minus_r[:], log_r[g][:], -1.0 / (4.0 * ALPHA))
-            unlift = stats.tile([P, GB], F32, name="unlift")
-            nc.vector.tensor_scalar(
-                unlift[:], log_root[g][:], -4.0 / (4.0 * ALPHA), 64.0 * math.log(2.0) / (4.0 * ALPHA), ALU.mult, ALU.add
-            )
-            minus_q = stats.tile([P, GB, SH], F32, name="minus_q")
-            nc.vector.scalar_tensor_tensor(
-                minus_q[:],
-                log_q[g][:],
-                -1.0 / (4.0 * ALPHA),
-                unlift[:].unsqueeze(2).to_broadcast([P, GB, SH]),
-                ALU.mult,
-                ALU.add,
-            )
 
             sa = last.tile([K, SH, GROUP], F32, name="sa")
             for i in range(SH):
-                zc = zc_psum.tile([K, GROUP], F32, name="zc")
-                nc.tensor.matmul(
-                    zc[:], cents_t[:, i * K : (i + 1) * K], pixels[:, g * GROUP : (g + 1) * GROUP], start=True, stop=False
-                )
+                zc = dot_products(g, i, stop=False)
                 for b in range(GB):
                     cols = slice(b * P, (b + 1) * P)
                     nc.tensor.matmul(
@@ -159,7 +163,7 @@ def tile_sralnet_kernel(tc, x, centroids, base, offs, out):
                     )
                     nc.tensor.matmul(
                         zc[:, cols],
-                        minus_q[:, b, i : i + 1].to_broadcast([P, K]),
+                        minus_q[:, g, b, i : i + 1].to_broadcast([P, K]),
                         ident_f[:],
                         is_transpose=True,
                         start=False,

@@ -6,6 +6,7 @@ from concourse.masks import make_identity
 F32 = mybir.dt.float32
 BF16 = mybir.dt.bfloat16
 U16 = mybir.dt.uint16
+I32 = mybir.dt.int32
 ALU = mybir.AluOpType
 ACT = mybir.ActivationFunctionType
 FREE_AXIS = mybir.AxisListType.X
@@ -16,7 +17,6 @@ P = 128
 GB = 4
 GROUP = GB * P
 GROUPS = N // GROUP
-LIFT = 2.0**32
 
 FLOPS = 2 * K * SH * D * N
 
@@ -48,7 +48,7 @@ def tile_sralnet_kernel(tc, x, centroids, base, offs, out):
         nc.vector.tensor_copy(ident_b[:], ident_f[:])
         ones_col = held.tile([K, 1], BF16, name="ones_col")
         nc.vector.memset(ones_col[:], 1.0)
-        half = held.tile([P, GROUPS, GB], F32, name="half")
+        half = held.tile([K, SH], F32, name="half")
         nc.vector.memset(half[:], 0.5)
 
         cents_t_ps = zc_psum.tile([D, SH * K], BF16, name="cents_t_ps", tag="zc")
@@ -62,7 +62,7 @@ def tile_sralnet_kernel(tc, x, centroids, base, offs, out):
             squares = work.tile([K, D], F32, name="squares")
             nc.scalar.activation(squares[:], cents[:, i, :], ACT.Square, accum_out=sumsq[:, i : i + 1])
         norm = held.tile([K, SH], F32, name="norm")
-        nc.gpsimd.tensor_tensor(norm[:], sumsq[:], half[:, 0, :SH], ALU.pow)
+        nc.gpsimd.tensor_tensor(norm[:], sumsq[:], half[:], ALU.pow)
         bias = held.tile([K, SH], F32, name="bias")
         nc.vector.tensor_scalar_mul(bias[:], norm[:], -ALPHA)
         twice_bias = held.tile([K, SH], F32, name="twice_bias")
@@ -116,29 +116,29 @@ def tile_sralnet_kernel(tc, x, centroids, base, offs, out):
 
         total = held.tile([P, GROUPS, GB], F32, name="total")
         nc.vector.tensor_reduce(total[:], sum_q[:], FREE_AXIS, ALU.add)
+        exponent = held.tile([P, GROUPS, GB], I32, name="exponent")
+        nc.vector.tensor_single_scalar(exponent[:], total[:].bitcast(I32), 23, ALU.logical_shift_right)
+        lift_exponent = held.tile([P, GROUPS, GB], I32, name="lift_exponent")
+        nc.vector.tensor_scalar(lift_exponent[:], exponent[:], -1.0, 286.0, ALU.mult, ALU.add)
         lift = held.tile([P, GROUPS, GB], F32, name="lift")
-        nc.vector.reciprocal(lift[:], total[:])
-        nc.vector.tensor_scalar_mul(lift[:], lift[:], LIFT)
+        nc.vector.tensor_single_scalar(lift[:].bitcast(I32), lift_exponent[:], 23, ALU.logical_shift_left)
         q_lifted = held.tile([P, GROUPS, GB, SH], F32, name="q_lifted")
         nc.vector.tensor_tensor(
             q_lifted[:], sum_q[:], lift[:].unsqueeze(3).to_broadcast([P, GROUPS, GB, SH]), ALU.mult
         )
-        root_total = held.tile([P, GROUPS, GB], F32, name="root_total")
-        nc.gpsimd.tensor_tensor(root_total[:], total[:], half[:], ALU.pow)
-
-        for g in range(GROUPS):
-            log_r[g] = work.tile([P, GB, K], F32, name="log_r")
-            for b in range(GB):
-                nc.scalar.activation(log_r[g][:, b, :], sum_r[g][:, b, :], ACT.Ln, scale=lift[:, g, b : b + 1])
-        log_q = held.tile([P, GROUPS, GB, SH], F32, name="log_q")
-        nc.scalar.activation(log_q[:], q_lifted[:], ACT.Ln)
-        log_root = held.tile([P, GROUPS, GB], F32, name="log_root")
-        nc.scalar.activation(log_root[:], root_total[:], ACT.Ln)
-
         unlift = held.tile([P, GROUPS, GB], F32, name="unlift")
         nc.vector.tensor_scalar(
-            unlift[:], log_root[:], -4.0 / (4.0 * ALPHA), 64.0 * math.log(2.0) / (4.0 * ALPHA), ALU.mult, ALU.add
+            unlift[:],
+            exponent[:],
+            -2.0 * math.log(2.0) / (4.0 * ALPHA),
+            2.0 * 159.0 * math.log(2.0) / (4.0 * ALPHA),
+            ALU.mult,
+            ALU.add,
         )
+
+        log_q = held.tile([P, GROUPS, GB, SH], F32, name="log_q")
+        nc.scalar.activation(log_q[:], q_lifted[:], ACT.Ln)
+
         minus_q = held.tile([P, GROUPS, GB, SH], F32, name="minus_q")
         nc.vector.scalar_tensor_tensor(
             minus_q[:],
@@ -148,6 +148,11 @@ def tile_sralnet_kernel(tc, x, centroids, base, offs, out):
             ALU.mult,
             ALU.add,
         )
+
+        for g in range(GROUPS):
+            log_r[g] = work.tile([P, GB, K], F32, name="log_r")
+            for b in range(GB):
+                nc.scalar.activation(log_r[g][:, b, :], sum_r[g][:, b, :], ACT.Ln, scale=lift[:, g, b : b + 1])
 
         for g in range(GROUPS):
             minus_r = work.tile([P, GB, K], F32, name="minus_r")
@@ -174,7 +179,7 @@ def tile_sralnet_kernel(tc, x, centroids, base, offs, out):
             factors = []
             for h in range(2):
                 odd = last.tile([K, GROUP], F32, name="odd")
-                nc.vector.tensor_scalar_add(odd[:], sa[:, 2 * h + 1, :], 1.0)
+                nc.scalar.add(odd[:], sa[:, 2 * h + 1, :], 1.0)
                 factor = last.tile([K, GROUP], F32, name=f"factor{h}")
                 nc.vector.scalar_tensor_tensor(factor[:], sa[:, 2 * h, :], 1.0, odd[:], ALU.add, ALU.mult)
                 factors.append(factor)

@@ -87,8 +87,8 @@ def tile_sralnet_kernel(tc, x, centroids, base, offs, out):
                 nc.vector.tensor_copy(e_rounded[g][:, i, :], e[g][:, i, :])
 
         def sums(g):
-            for b in range(GB):
-                for i in range(SH):
+            for i in range(SH):
+                for b in range(GB):
                     nc.tensor.matmul(
                         sum_q[:, g, b, i : i + 1],
                         e_rounded[g][:, i, b * P : (b + 1) * P],
@@ -96,16 +96,19 @@ def tile_sralnet_kernel(tc, x, centroids, base, offs, out):
                         start=True,
                         stop=True,
                     )
+            pairs = work.tile([K, 2, GROUP], F32, name="pairs")
+            for h in range(2):
+                nc.vector.tensor_tensor(pairs[:, h, :], e[g][:, 2 * h, :], e[g][:, 2 * h + 1, :], ALU.add)
             sum_r[g] = r_psum.tile([P, GB, K], F32, name="sum_r")
-            for b in range(GB):
-                for i in range(SH):
+            for h in range(2):
+                for b in range(GB):
                     nc.tensor.matmul(
                         sum_r[g][:, b, :],
-                        e[g][:, i, b * P : (b + 1) * P],
+                        pairs[:, h, b * P : (b + 1) * P],
                         ident_f[:],
                         is_transpose=True,
-                        start=(i == 0),
-                        stop=(i == SH - 1),
+                        start=(h == 0 and b == 0),
+                        stop=(h == 1 and b == GB - 1),
                     )
 
         exponentials(0)
@@ -116,12 +119,10 @@ def tile_sralnet_kernel(tc, x, centroids, base, offs, out):
 
         total = held.tile([P, GROUPS, GB], F32, name="total")
         nc.vector.tensor_reduce(total[:], sum_q[:], FREE_AXIS, ALU.add)
-        exponent = held.tile([P, GROUPS, GB], I32, name="exponent")
-        nc.vector.tensor_single_scalar(exponent[:], total[:].bitcast(I32), 23, ALU.logical_shift_right)
-        lift_exponent = held.tile([P, GROUPS, GB], I32, name="lift_exponent")
-        nc.vector.tensor_scalar(lift_exponent[:], exponent[:], -1.0, 286.0, ALU.mult, ALU.add)
+        field = held.tile([P, GROUPS, GB], I32, name="field")
+        nc.vector.tensor_single_scalar(field[:], total[:].bitcast(I32), 0x7F800000, ALU.bitwise_and)
         lift = held.tile([P, GROUPS, GB], F32, name="lift")
-        nc.vector.tensor_single_scalar(lift[:].bitcast(I32), lift_exponent[:], 23, ALU.logical_shift_left)
+        nc.vector.tensor_scalar(lift[:].bitcast(I32), field[:], -1.0, 286.0 * 2.0**23, ALU.mult, ALU.add)
         q_lifted = held.tile([P, GROUPS, GB, SH], F32, name="q_lifted")
         nc.vector.tensor_tensor(
             q_lifted[:], sum_q[:], lift[:].unsqueeze(3).to_broadcast([P, GROUPS, GB, SH]), ALU.mult
@@ -129,8 +130,8 @@ def tile_sralnet_kernel(tc, x, centroids, base, offs, out):
         unlift = held.tile([P, GROUPS, GB], F32, name="unlift")
         nc.vector.tensor_scalar(
             unlift[:],
-            exponent[:],
-            -2.0 * math.log(2.0) / (4.0 * ALPHA),
+            field[:],
+            -2.0 * math.log(2.0) / (4.0 * ALPHA) / 2.0**23,
             2.0 * 159.0 * math.log(2.0) / (4.0 * ALPHA),
             ALU.mult,
             ALU.add,

@@ -18,6 +18,8 @@ GB = 4
 GROUP = GB * P
 GROUPS = N // GROUP
 
+ODD_FIRST = (1, 0, 3, 2)
+
 FLOPS = 2 * K * SH * D * N
 
 
@@ -160,7 +162,7 @@ def tile_sralnet_kernel(tc, x, centroids, base, offs, out):
             nc.vector.tensor_scalar_mul(minus_r[:], log_r[g][:], -1.0 / (4.0 * ALPHA))
 
             sa = last.tile([K, SH, GROUP], F32, name="sa")
-            for i in range(SH):
+            for i in ODD_FIRST:
                 zc = dot_products(g, i, stop=False)
                 for b in range(GB):
                     cols = slice(b * P, (b + 1) * P)
@@ -180,7 +182,10 @@ def tile_sralnet_kernel(tc, x, centroids, base, offs, out):
             factors = []
             for h in range(2):
                 odd = last.tile([K, GROUP], F32, name="odd")
-                nc.scalar.add(odd[:], sa[:, 2 * h + 1, :], 1.0)
+                if g == 0:
+                    nc.vector.tensor_scalar_add(odd[:], sa[:, 2 * h + 1, :], 1.0)
+                else:
+                    nc.scalar.add(odd[:], sa[:, 2 * h + 1, :], 1.0)
                 factor = last.tile([K, GROUP], F32, name=f"factor{h}")
                 nc.vector.scalar_tensor_tensor(factor[:], sa[:, 2 * h, :], 1.0, odd[:], ALU.add, ALU.mult)
                 factors.append(factor)

@@ -66,9 +66,9 @@ def tile_sralnet_kernel(tc, x, centroids, base, offs, out):
         norm = held.tile([K, SH], F32, name="norm")
         nc.gpsimd.tensor_tensor(norm[:], sumsq[:], half[:], ALU.pow)
         bias = held.tile([K, SH], F32, name="bias")
-        nc.vector.tensor_scalar_mul(bias[:], norm[:], -ALPHA)
+        nc.gpsimd.tensor_scalar_mul(bias[:], norm[:], -ALPHA)
         twice_bias = held.tile([K, SH], F32, name="twice_bias")
-        nc.vector.tensor_scalar_mul(twice_bias[:], norm[:], -2.0 * ALPHA)
+        nc.gpsimd.tensor_scalar_mul(twice_bias[:], norm[:], -2.0 * ALPHA)
 
         def dot_products(g, i, stop):
             zc = zc_psum.tile([K, GROUP], F32, name="zc")
@@ -113,11 +113,10 @@ def tile_sralnet_kernel(tc, x, centroids, base, offs, out):
                         stop=(h == 1 and b == GB - 1),
                     )
 
-        exponentials(0)
-        for g in range(1, GROUPS):
+        for g in range(GROUPS):
             exponentials(g)
-            sums(g - 1)
-        sums(GROUPS - 1)
+        for g in range(GROUPS):
+            sums(g)
 
         total = held.tile([P, GROUPS, GB], F32, name="total")
         nc.vector.tensor_reduce(total[:], sum_q[:], FREE_AXIS, ALU.add)

@@ -18,8 +18,6 @@ GB = 4
 GROUP = GB * P
 GROUPS = N // GROUP
 
-ODD_FIRST = (1, 0, 3, 2)
-
 FLOPS = 2 * K * SH * D * N
 
 
@@ -28,9 +26,8 @@ def tile_sralnet_kernel(tc, x, centroids, base, offs, out):
     with (
         tc.tile_pool(name="held", bufs=1) as held,
         tc.tile_pool(name="work", bufs=GROUPS) as work,
-        tc.tile_pool(name="last", bufs=2) as last,
-        tc.psum_pool(name="zc_psum", bufs=3) as zc_psum,
-        tc.psum_pool(name="r_psum", bufs=GROUPS) as r_psum,
+        tc.tile_pool(name="last", bufs=3) as last,
+        tc.psum_pool(name="banks", bufs=7) as banks,
         tc.psum_pool(name="q_psum", bufs=1) as q_psum,
     ):
         cents = held.tile([K, SH, D], BF16, name="cents")
@@ -53,25 +50,30 @@ def tile_sralnet_kernel(tc, x, centroids, base, offs, out):
         half = held.tile([K, SH], F32, name="half")
         nc.vector.memset(half[:], 0.5)
 
-        cents_t_ps = zc_psum.tile([D, SH * K], BF16, name="cents_t_ps", tag="zc")
-        for i in range(SH):
-            nc.tensor.transpose(cents_t_ps[:, i * K : (i + 1) * K], cents[:, i, :], ident_b[:])
         cents_t = held.tile([D, SH * K], BF16, name="cents_t")
-        nc.vector.tensor_copy(cents_t[:], cents_t_ps[:])
+        for i in range(SH):
+            cents_t_ps = banks.tile([D, K], BF16, name="cents_t_ps", tag="bank")
+            nc.tensor.transpose(cents_t_ps[:], cents[:, i, :], ident_b[:])
+            nc.vector.tensor_copy(cents_t[:, i * K : (i + 1) * K], cents_t_ps[:])
 
         sumsq = held.tile([K, SH], F32, name="sumsq")
-        for i in range(SH):
-            squares = work.tile([K, D], F32, name="squares")
-            nc.scalar.activation(squares[:], cents[:, i, :], ACT.Square, accum_out=sumsq[:, i : i + 1])
         norm = held.tile([K, SH], F32, name="norm")
-        nc.gpsimd.tensor_tensor(norm[:], sumsq[:], half[:], ALU.pow)
         bias = held.tile([K, SH], F32, name="bias")
-        nc.gpsimd.tensor_scalar_mul(bias[:], norm[:], -ALPHA)
+        for first in range(0, SH, 2):
+            two = slice(first, first + 2)
+            for i in range(first, first + 2):
+                squares = work.tile([K, D], F32, name="squares")
+                nc.scalar.activation(squares[:], cents[:, i, :], ACT.Square, accum_out=sumsq[:, i : i + 1])
+            nc.gpsimd.tensor_tensor(norm[:, two], sumsq[:, two], half[:, two], ALU.pow)
+            if first == 0:
+                nc.scalar.mul(bias[:, two], norm[:, two], -ALPHA)
+            else:
+                nc.gpsimd.tensor_scalar_mul(bias[:, two], norm[:, two], -ALPHA)
         twice_bias = held.tile([K, SH], F32, name="twice_bias")
         nc.gpsimd.tensor_scalar_mul(twice_bias[:], norm[:], -2.0 * ALPHA)
 
         def dot_products(g, i, stop):
-            zc = zc_psum.tile([K, GROUP], F32, name="zc")
+            zc = banks.tile([K, GROUP], F32, name="zc", tag="bank")
             nc.tensor.matmul(
                 zc[:], cents_t[:, i * K : (i + 1) * K], pixels[:, g * GROUP : (g + 1) * GROUP], start=True, stop=stop
             )
@@ -101,7 +103,7 @@ def tile_sralnet_kernel(tc, x, centroids, base, offs, out):
             pairs = work.tile([K, 2, GROUP], F32, name="pairs")
             for h in range(2):
                 nc.vector.tensor_tensor(pairs[:, h, :], e[g][:, 2 * h, :], e[g][:, 2 * h + 1, :], ALU.add)
-            sum_r[g] = r_psum.tile([P, GB, K], F32, name="sum_r")
+            sum_r[g] = banks.tile([P, GB, K], F32, name="sum_r", tag="bank")
             for h in range(2):
                 for b in range(GB):
                     nc.tensor.matmul(
@@ -156,17 +158,15 @@ def tile_sralnet_kernel(tc, x, centroids, base, offs, out):
             for b in range(GB):
                 nc.scalar.activation(log_r[g][:, b, :], sum_r[g][:, b, :], ACT.Ln, scale=lift[:, g, b : b + 1])
 
-        for g in range(GROUPS):
-            minus_r = work.tile([P, GB, K], F32, name="minus_r")
-            nc.vector.tensor_scalar_mul(minus_r[:], log_r[g][:], -1.0 / (4.0 * ALPHA))
+        minus_r, sa, factors = {}, {}, {}
 
-            sa = last.tile([K, SH, GROUP], F32, name="sa")
-            for i in ODD_FIRST:
+        def half_of_m(g, h):
+            for i in (2 * h + 1, 2 * h):
                 zc = dot_products(g, i, stop=False)
                 for b in range(GB):
                     cols = slice(b * P, (b + 1) * P)
                     nc.tensor.matmul(
-                        zc[:, cols], minus_r[:, b, :], ident_f[:], is_transpose=True, start=False, stop=False
+                        zc[:, cols], minus_r[g][:, b, :], ident_f[:], is_transpose=True, start=False, stop=False
                     )
                     nc.tensor.matmul(
                         zc[:, cols],
@@ -176,22 +176,31 @@ def tile_sralnet_kernel(tc, x, centroids, base, offs, out):
                         start=False,
                         stop=(b == GB - 1),
                     )
-                nc.scalar.activation(sa[:, i, :], zc[:], ACT.Exp, scale=4.0 * ALPHA, bias=twice_bias[:, i : i + 1])
+                nc.scalar.activation(
+                    sa[g][:, i, :], zc[:], ACT.Exp, scale=4.0 * ALPHA, bias=twice_bias[:, i : i + 1]
+                )
+            odd = last.tile([K, GROUP], F32, name="odd")
+            if g == 0:
+                nc.vector.tensor_scalar_add(odd[:], sa[g][:, 2 * h + 1, :], 1.0)
+            else:
+                nc.scalar.add(odd[:], sa[g][:, 2 * h + 1, :], 1.0)
+            factors[g, h] = last.tile([K, GROUP], F32, name=f"factor{h}")
+            nc.vector.scalar_tensor_tensor(factors[g, h][:], sa[g][:, 2 * h, :], 1.0, odd[:], ALU.add, ALU.mult)
 
-            factors = []
-            for h in range(2):
-                odd = last.tile([K, GROUP], F32, name="odd")
-                if g == 0:
-                    nc.vector.tensor_scalar_add(odd[:], sa[:, 2 * h + 1, :], 1.0)
-                else:
-                    nc.scalar.add(odd[:], sa[:, 2 * h + 1, :], 1.0)
-                factor = last.tile([K, GROUP], F32, name=f"factor{h}")
-                nc.vector.scalar_tensor_tensor(factor[:], sa[:, 2 * h, :], 1.0, odd[:], ALU.add, ALU.mult)
-                factors.append(factor)
-
+        def scatter(g):
             list_cols = slice(g * GROUP // 16, (g + 1) * GROUP // 16)
             nc.vector.tensor_tensor(
-                window[:].indirect(offsets[:, list_cols]), factors[0][:], factors[1][:], ALU.mult
+                window[:].indirect(offsets[:, list_cols]), factors[g, 0][:], factors[g, 1][:], ALU.mult
             )
+
+        for g in range(GROUPS):
+            minus_r[g] = work.tile([P, GB, K], F32, name="minus_r")
+            nc.vector.tensor_scalar_mul(minus_r[g][:], log_r[g][:], -1.0 / (4.0 * ALPHA))
+            sa[g] = last.tile([K, SH, GROUP], F32, name="sa")
+            half_of_m(g, 0)
+            if g > 0:
+                scatter(g - 1)
+            half_of_m(g, 1)
+        scatter(GROUPS - 1)
 
         nc.sync.dma_start(out, window[:])

@@ -13,6 +13,7 @@ FREE_AXIS = mybir.AxisListType.X
 
 K, SH, D, S, N = 128, 4, 128, 4096, 2048
 ALPHA = 100.0
+SMALL = 2.0**-31
 P = 128
 GB = 4
 GROUP = GB * P
@@ -45,8 +46,8 @@ def tile_sralnet_kernel(tc, x, centroids, base, offs, out):
         make_identity(nc, ident_f[:])
         ident_b = held.tile([P, P], BF16, name="ident_b")
         nc.vector.tensor_copy(ident_b[:], ident_f[:])
-        ones_col = held.tile([K, 1], BF16, name="ones_col")
-        nc.vector.memset(ones_col[:], 1.0)
+        small_col = held.tile([K, 1], BF16, name="small_col")
+        nc.vector.memset(small_col[:], SMALL)
         half = held.tile([K, SH], F32, name="half")
         nc.vector.memset(half[:], 0.5)
 
@@ -96,7 +97,7 @@ def tile_sralnet_kernel(tc, x, centroids, base, offs, out):
                     nc.tensor.matmul(
                         sum_q[:, g, b, i : i + 1],
                         e_rounded[g][:, i, b * P : (b + 1) * P],
-                        ones_col[:],
+                        small_col[:],
                         start=True,
                         stop=True,
                     )
@@ -122,10 +123,10 @@ def tile_sralnet_kernel(tc, x, centroids, base, offs, out):
 
         total = held.tile([P, GROUPS, GB], F32, name="total")
         nc.vector.tensor_reduce(total[:], sum_q[:], FREE_AXIS, ALU.add)
-        field = held.tile([P, GROUPS, GB], I32, name="field")
-        nc.vector.tensor_single_scalar(field[:], total[:].bitcast(I32), 0x7F800000, ALU.bitwise_and)
         lift = held.tile([P, GROUPS, GB], F32, name="lift")
-        nc.vector.tensor_scalar(lift[:].bitcast(I32), field[:], -1.0, 286.0 * 2.0**23, ALU.mult, ALU.add)
+        nc.vector.tensor_scalar(
+            lift[:].bitcast(I32), total[:].bitcast(I32), 0x7F800000, 0x7F800000, ALU.bitwise_and, ALU.bitwise_xor
+        )
         q_lifted = held.tile([P, GROUPS, GB, SH], F32, name="q_lifted")
         nc.vector.tensor_tensor(
             q_lifted[:], sum_q[:], lift[:].unsqueeze(3).to_broadcast([P, GROUPS, GB, SH]), ALU.mult
@@ -133,15 +134,15 @@ def tile_sralnet_kernel(tc, x, centroids, base, offs, out):
         unlift = held.tile([P, GROUPS, GB], F32, name="unlift")
         nc.vector.tensor_scalar(
             unlift[:],
-            field[:],
-            -2.0 * math.log(2.0) / (4.0 * ALPHA) / 2.0**23,
-            2.0 * 159.0 * math.log(2.0) / (4.0 * ALPHA),
+            lift[:].bitcast(I32),
+            2.0 * math.log(2.0) / (4.0 * ALPHA) / 2.0**23,
+            -2.0 * 127.0 * math.log(2.0) / (4.0 * ALPHA),
             ALU.mult,
             ALU.add,
         )
 
         log_q = held.tile([P, GROUPS, GB, SH], F32, name="log_q")
-        nc.scalar.activation(log_q[:], q_lifted[:], ACT.Ln)
+        nc.scalar.activation(log_q[:], q_lifted[:], ACT.Ln, scale=1.0 / SMALL)
 
         minus_q = held.tile([P, GROUPS, GB, SH], F32, name="minus_q")
         nc.vector.scalar_tensor_tensor(

@@ -27,7 +27,7 @@ def tile_sralnet_kernel(tc, x, centroids, base, offs, out):
     with (
         tc.tile_pool(name="held", bufs=1) as held,
         tc.tile_pool(name="work", bufs=GROUPS) as work,
-        tc.tile_pool(name="last", bufs=3) as last,
+        tc.tile_pool(name="last", bufs=GROUPS) as last,
         tc.psum_pool(name="banks", bufs=7) as banks,
         tc.psum_pool(name="q_psum", bufs=1) as q_psum,
     ):

@@ -91,7 +91,7 @@ def tile_sralnet_kernel(tc, x, centroids, base, offs, out):
                 nc.scalar.activation(e[g][:, i, :], zc[:], ACT.Exp, scale=2.0 * ALPHA, bias=bias[:, i : i + 1])
                 nc.vector.tensor_copy(e_rounded[g][:, i, :], e[g][:, i, :])
 
-        def sums(g):
+        def sums_over_clusters(g):
             for i in range(SH):
                 for b in range(GB):
                     nc.tensor.matmul(
@@ -101,6 +101,8 @@ def tile_sralnet_kernel(tc, x, centroids, base, offs, out):
                         start=True,
                         stop=True,
                     )
+
+        def sums_over_shadows(g):
             pairs = work.tile([K, 2, GROUP], F32, name="pairs")
             for h in range(2):
                 nc.vector.tensor_tensor(pairs[:, h, :], e[g][:, 2 * h, :], e[g][:, 2 * h + 1, :], ALU.add)
@@ -118,8 +120,12 @@ def tile_sralnet_kernel(tc, x, centroids, base, offs, out):
 
         for g in range(GROUPS):
             exponentials(g)
-        for g in range(GROUPS):
-            sums(g)
+        for g in range(GROUPS - 1):
+            sums_over_clusters(g)
+            sums_over_shadows(g)
+        sums_over_clusters(GROUPS - 1)
+        early = {i: dot_products(0, i, stop=False) for i in (1, 0, 3)}
+        sums_over_shadows(GROUPS - 1)
 
         total = held.tile([P, GROUPS, GB], F32, name="total")
         nc.vector.tensor_reduce(total[:], sum_q[:], FREE_AXIS, ALU.add)
@@ -163,7 +169,7 @@ def tile_sralnet_kernel(tc, x, centroids, base, offs, out):
 
         def half_of_m(g, h):
             for i in (2 * h + 1, 2 * h):
-                zc = dot_products(g, i, stop=False)
+                zc = early[i] if g == 0 and i in early else dot_products(g, i, stop=False)
                 for b in range(GB):
                     cols = slice(b * P, (b + 1) * P)
                     nc.tensor.matmul(

import math

import concourse.mybir as mybir
from concourse.masks import make_identity

F32 = mybir.dt.float32
BF16 = mybir.dt.bfloat16
U16 = mybir.dt.uint16
I32 = mybir.dt.int32
ALU = mybir.AluOpType
ACT = mybir.ActivationFunctionType
FREE_AXIS = mybir.AxisListType.X

K, SH, D, S, N = 128, 4, 128, 4096, 2048
ALPHA = 100.0
SMALL = 2.0**-31
P = 128
GB = 4
GROUP = GB * P
GROUPS = N // GROUP

FLOPS = 2 * K * SH * D * N


def tile_sralnet_kernel(tc, x, centroids, base, offs, out):
    nc = tc.nc
    with (
        tc.tile_pool(name="held", bufs=1) as held,
        tc.tile_pool(name="work", bufs=GROUPS) as work,
        tc.tile_pool(name="last", bufs=GROUPS) as last,
        tc.psum_pool(name="banks", bufs=7) as banks,
        tc.psum_pool(name="q_psum", bufs=1) as q_psum,
    ):
        cents = held.tile([K, SH, D], BF16, name="cents")
        nc.sync.dma_start(cents[:], centroids)
        pixels = held.tile([D, N], BF16, name="pixels")
        for g in range(GROUPS):
            cols = slice(g * GROUP, (g + 1) * GROUP)
            nc.sync.dma_start(pixels[:, cols], x[:, cols])
        offsets = held.tile([P, N // 16], U16, name="offsets")
        nc.sync.dma_start(offsets[:], offs)
        window = held.tile([K, S], F32, name="window")
        nc.sync.dma_start(window[:], base)

        ident_f = held.tile([P, P], F32, name="ident_f")
        make_identity(nc, ident_f[:])
        ident_b = held.tile([P, P], BF16, name="ident_b")
        nc.vector.tensor_copy(ident_b[:], ident_f[:])
        small_col = held.tile([K, 1], BF16, name="small_col")
        nc.vector.memset(small_col[:], SMALL)
        half = held.tile([K, SH], F32, name="half")
        nc.vector.memset(half[:], 0.5)

        cents_t = held.tile([D, SH * K], BF16, name="cents_t")
        for i in range(SH):
            cents_t_ps = banks.tile([D, K], BF16, name="cents_t_ps", tag="bank")
            nc.tensor.transpose(cents_t_ps[:], cents[:, i, :], ident_b[:])
            nc.vector.tensor_copy(cents_t[:, i * K : (i + 1) * K], cents_t_ps[:])

        sumsq = held.tile([K, SH], F32, name="sumsq")
        norm = held.tile([K, SH], F32, name="norm")
        bias = held.tile([K, SH], F32, name="bias")
        for first in range(0, SH, 2):
            two = slice(first, first + 2)
            for i in range(first, first + 2):
                squares = work.tile([K, D], F32, name="squares")
                nc.scalar.activation(squares[:], cents[:, i, :], ACT.Square, accum_out=sumsq[:, i : i + 1])
            nc.gpsimd.tensor_tensor(norm[:, two], sumsq[:, two], half[:, two], ALU.pow)
            if first == 0:
                nc.scalar.mul(bias[:, two], norm[:, two], -ALPHA)
            else:
                nc.gpsimd.tensor_scalar_mul(bias[:, two], norm[:, two], -ALPHA)
        twice_bias = held.tile([K, SH], F32, name="twice_bias")
        nc.gpsimd.tensor_scalar_mul(twice_bias[:], norm[:], -2.0 * ALPHA)

        def dot_products(g, i, stop):
            zc = banks.tile([K, GROUP], F32, name="zc", tag="bank")
            nc.tensor.matmul(
                zc[:], cents_t[:, i * K : (i + 1) * K], pixels[:, g * GROUP : (g + 1) * GROUP], start=True, stop=stop
            )
            return zc

        e, e_rounded, sum_r, log_r = {}, {}, {}, {}
        sum_q = q_psum.tile([P, GROUPS, GB, SH], F32, name="sum_q")

        def exponentials(g):
            e[g] = work.tile([K, SH, GROUP], F32, name="e")
            e_rounded[g] = work.tile([K, SH, GROUP], BF16, name="e_rounded")
            for i in range(SH):
                zc = dot_products(g, i, stop=True)
                nc.scalar.activation(e[g][:, i, :], zc[:], ACT.Exp, scale=2.0 * ALPHA, bias=bias[:, i : i + 1])
                nc.vector.tensor_copy(e_rounded[g][:, i, :], e[g][:, i, :])

        def sums_over_clusters(g):
            for i in range(SH):
                for b in range(GB):
                    nc.tensor.matmul(
                        sum_q[:, g, b, i : i + 1],
                        e_rounded[g][:, i, b * P : (b + 1) * P],
                        small_col[:],
                        start=True,
                        stop=True,
                    )

        def sums_over_shadows(g):
            pairs = work.tile([K, 2, GROUP], F32, name="pairs")
            for h in range(2):
                nc.vector.tensor_tensor(pairs[:, h, :], e[g][:, 2 * h, :], e[g][:, 2 * h + 1, :], ALU.add)
            sum_r[g] = banks.tile([P, GB, K], F32, name="sum_r", tag="bank")
            for h in range(2):
                for b in range(GB):
                    nc.tensor.matmul(
                        sum_r[g][:, b, :],
                        pairs[:, h, b * P : (b + 1) * P],
                        ident_f[:],
                        is_transpose=True,
                        start=(h == 0 and b == 0),
                        stop=(h == 1 and b == GB - 1),
                    )

        for g in range(GROUPS):
            exponentials(g)
        for g in range(GROUPS - 1):
            sums_over_clusters(g)
            sums_over_shadows(g)
        sums_over_clusters(GROUPS - 1)
        early = {i: dot_products(0, i, stop=False) for i in (1, 0, 3)}
        sums_over_shadows(GROUPS - 1)

        total = held.tile([P, GROUPS, GB], F32, name="total")
        nc.vector.tensor_reduce(total[:], sum_q[:], FREE_AXIS, ALU.add)
        lift = held.tile([P, GROUPS, GB], F32, name="lift")
        nc.vector.tensor_scalar(
            lift[:].bitcast(I32), total[:].bitcast(I32), 0x7F800000, 0x7F800000, ALU.bitwise_and, ALU.bitwise_xor
        )
        q_lifted = held.tile([P, GROUPS, GB, SH], F32, name="q_lifted")
        nc.vector.tensor_tensor(
            q_lifted[:], sum_q[:], lift[:].unsqueeze(3).to_broadcast([P, GROUPS, GB, SH]), ALU.mult
        )
        unlift = held.tile([P, GROUPS, GB], F32, name="unlift")
        nc.vector.tensor_scalar(
            unlift[:],
            lift[:].bitcast(I32),
            2.0 * math.log(2.0) / (4.0 * ALPHA) / 2.0**23,
            -2.0 * 127.0 * math.log(2.0) / (4.0 * ALPHA),
            ALU.mult,
            ALU.add,
        )

        log_q = held.tile([P, GROUPS, GB, SH], F32, name="log_q")
        nc.scalar.activation(log_q[:], q_lifted[:], ACT.Ln, scale=1.0 / SMALL)

        minus_q = held.tile([P, GROUPS, GB, SH], F32, name="minus_q")
        nc.vector.scalar_tensor_tensor(
            minus_q[:],
            log_q[:],
            -1.0 / (4.0 * ALPHA),
            unlift[:].unsqueeze(3).to_broadcast([P, GROUPS, GB, SH]),
            ALU.mult,
            ALU.add,
        )

        for g in range(GROUPS):
            log_r[g] = work.tile([P, GB, K], F32, name="log_r")
            for b in range(GB):
                nc.scalar.activation(log_r[g][:, b, :], sum_r[g][:, b, :], ACT.Ln, scale=lift[:, g, b : b + 1])

        minus_r, sa, factors = {}, {}, {}

        def half_of_m(g, h):
            for i in (2 * h + 1, 2 * h):
                zc = early[i] if g == 0 and i in early else dot_products(g, i, stop=False)
                for b in range(GB):
                    cols = slice(b * P, (b + 1) * P)
                    nc.tensor.matmul(
                        zc[:, cols], minus_r[g][:, b, :], ident_f[:], is_transpose=True, start=False, stop=False
                    )
                    nc.tensor.matmul(
                        zc[:, cols],
                        minus_q[:, g, b, i : i + 1].to_broadcast([P, K]),
                        ident_f[:],
                        is_transpose=True,
                        start=False,
                        stop=(b == GB - 1),
                    )
                nc.scalar.activation(
                    sa[g][:, i, :], zc[:], ACT.Exp, scale=4.0 * ALPHA, bias=twice_bias[:, i : i + 1]
                )
            odd = last.tile([K, GROUP], F32, name="odd")
            if g == 0:
                nc.vector.tensor_scalar_add(odd[:], sa[g][:, 2 * h + 1, :], 1.0)
            else:
                nc.scalar.add(odd[:], sa[g][:, 2 * h + 1, :], 1.0)
            factors[g, h] = last.tile([K, GROUP], F32, name=f"factor{h}")
            nc.vector.scalar_tensor_tensor(factors[g, h][:], sa[g][:, 2 * h, :], 1.0, odd[:], ALU.add, ALU.mult)

        def scatter(g):
            list_cols = slice(g * GROUP // 16, (g + 1) * GROUP // 16)
            nc.vector.tensor_tensor(
                window[:].indirect(offsets[:, list_cols]), factors[g, 0][:], factors[g, 1][:], ALU.mult
            )

        for g in range(GROUPS):
            minus_r[g] = work.tile([P, GB, K], F32, name="minus_r")
            nc.vector.tensor_scalar_mul(minus_r[g][:], log_r[g][:], -1.0 / (4.0 * ALPHA))
            sa[g] = last.tile([K, SH, GROUP], F32, name="sa")
            half_of_m(g, 0)
            if g > 0:
                scatter(g - 1)
            half_of_m(g, 1)
        scatter(GROUPS - 1)

        nc.sync.dma_start(out, window[:])
